import numpy as np
import ml_dtypes


def mxq(x, axis, fmt="e4m3"):
    dtype, down = {"e4m3": (ml_dtypes.float8_e4m3fn, 7), "e5m2": (ml_dtypes.float8_e5m2, 14)}[fmt]
    v = np.moveaxis(np.asarray(x, np.float32).astype(ml_dtypes.bfloat16).astype(np.float64), axis, -1)
    blocks = v.reshape(v.shape[:-1] + (-1, 32))
    amax = np.abs(blocks).max(-1, keepdims=True)
    byte = np.maximum(np.where(amax > 0, np.frexp(amax)[1] - 1 + 127, 0) - down, 1)
    scale = np.exp2(byte - 127.0)
    codes = (blocks / scale).astype(np.float32).astype(dtype).astype(np.float64)
    return np.moveaxis((codes * scale).reshape(v.shape), -1, axis)


WIDE = False


def mx_kscale(k):
    if not WIDE:
        return np.ones(k)
    levels = np.array([18, -18])
    if k % 512:
        return np.exp2(np.random.permutation(np.resize(levels, k // 32))).repeat(32)
    a = np.empty((k // 512, 16))
    for p in range(k // 512):
        a[p, :8] = np.random.permutation(np.resize(levels, 8))
        for g in range(8):
            far = levels[np.abs(levels - a[p, g]) >= 10]
            a[p, g + 8] = far[np.random.randint(len(far))]
    return np.exp2(a.ravel()).repeat(32)


BF16 = ml_dtypes.bfloat16


def bf(x):
    return np.asarray(x, np.float32).astype(BF16)


def f64(x):
    return np.asarray(x).astype(np.float64)


S, D, NH, HD = 1024, 1024, 8, 128
F = NH * HD
EPS = 1e-6
ROPE_BASE = 10000.0


def rope_tables():
    inv_freq = 1.0 / ROPE_BASE ** (np.arange(0, HD, 2) / HD)
    ang = np.arange(S)[:, None] * inv_freq[None, :]
    return np.cos(ang), np.sin(ang)


def rope_back(g, cos, sin):
    gp = g.reshape(S, NH, HD // 2, 2)
    ge, go = gp[..., 0], gp[..., 1]
    c, s = cos[:, None, :], sin[:, None, :]
    return np.stack([ge * c + go * s, go * c - ge * s], axis=-1).reshape(S, NH, HD)


def setup_inputs():
    s = mx_kscale(S)[:, None]
    uq = mx_kscale(F)
    uk = mx_kscale(F)
    sc = 1.0 / np.sqrt(D)
    row_gain = np.exp2(np.random.uniform(-11, 1, (S, 1)))
    x0 = bf(np.random.standard_normal((S, D)) * row_gain)
    norm_w = bf(1.0 + 0.1 * np.random.standard_normal(D))
    wq0 = bf(np.random.standard_normal((D, NH, HD)) * sc)
    wk0 = bf(np.random.standard_normal((D, NH, HD)) * sc)
    g0 = np.random.standard_normal((S, NH, HD)) * np.exp2(np.random.randint(-6, 1, (S, 1, 1))) * 0.25
    g1 = np.random.standard_normal((S, NH, HD)) * np.exp2(np.random.randint(-6, 1, (S, 1, 1))) * 0.25
    xf = f64(x0)
    rstd = 1.0 / np.sqrt(np.mean(xf * xf, axis=-1, keepdims=True) + EPS)
    return {"xs": bf(f64(x0) * s),
            "norm_w": norm_w,
            "wq": bf(f64(wq0) / uq.reshape(1, NH, HD)),
            "wk": bf(f64(wk0) / uk.reshape(1, NH, HD)),
            "rstd": np.asarray(rstd, np.float32),
            "grad_0": bf(g0 / s[:, :, None] * uq.reshape(1, NH, HD)),
            "grad_1": bf(g1 / s[:, :, None] * uk.reshape(1, NH, HD))}


def reference(xs, norm_w, wq, wk, rstd, grad_0, grad_1):
    x, gain, r = f64(xs), f64(norm_w), f64(rstd)
    cos, sin = rope_tables()
    dq = rope_back(f64(grad_0), cos, sin).reshape(S, F)
    dk = rope_back(f64(grad_1), cos, sin).reshape(S, F)
    dqk = np.concatenate([dq, dk], axis=1)
    w = np.concatenate([f64(wq).reshape(D, F), f64(wk).reshape(D, F)], axis=1)
    xhat = x * r
    h = xhat * gain
    dh = mxq(dqk, 1, "e5m2") @ mxq(w, 1, "e4m3").T
    dw = mxq(h, 0, "e4m3").T @ mxq(dqk, 0, "e5m2")
    t = dh * gain
    dxs = r * (t - xhat * np.mean(t * xhat, axis=-1, keepdims=True))
    return dxs, dw[:, :F].reshape(D, NH, HD), dw[:, F:].reshape(D, NH, HD)

@@ -1,0 +1,427 @@
+import math
+from contextlib import ExitStack
+
+import concourse.mybir as mybir
+from concourse.masks import make_identity
+
+S, D, NH, HD = 1024, 1024, 8, 128
+F = NH * HD
+ROPE_BASE = 10000.0
+FLOPS = 2 * 2 * S * D * 2 * F
+
+F32 = mybir.dt.float32
+BF16 = mybir.dt.bfloat16
+I32 = mybir.dt.int32
+U32 = mybir.dt.uint32
+U8 = mybir.dt.uint8
+E4M3 = mybir.dt.float8_e4m3fn_x4
+E5M2 = mybir.dt.float8_e5m2_x4
+ALU = mybir.AluOpType
+ACT = mybir.ActivationFunctionType
+AX = mybir.AxisListType
+
+P = 128
+PASS = 512
+PAIRS = HD // 2
+
+
+def tile_attentionmodule_pa_v_kernel(tc, xs, norm_w, wq, wk, rstd, grad_0, grad_1, out_0, out_1, out_2):
+    nc = tc.nc
+    with ExitStack() as ctx:
+        sb = ctx.enter_context(tc.tile_pool(name="sb", bufs=1))
+        ps = ctx.enter_context(tc.psum_pool(name="ps", bufs=1))
+        ctx.enter_context(tc.manual_schedule())
+
+        def sbuf(shape, dtype, tag, bufs=1):
+            return sb.tile(shape, dtype, name=tag, tag=tag, bufs=bufs, align_bytes=64)
+
+        def bank(b, dtype=F32):
+            width = PASS if dtype == F32 else 2 * PASS
+            return ps.tile([P, width], dtype, name="bank%d" % b, tag="bank%d" % b)
+
+        grads = [t.rearrange("(g p j) n h -> g p j (n h)", p=P, j=4) for t in (grad_0, grad_1)]
+        weights = [t.rearrange("(k p) n h -> p k (n h)", p=P) for t in (wq, wk)]
+        dws = [t.rearrange("(k p) n h -> p k (n h)", p=P) for t in (out_1, out_2)]
+        x_hbm = xs.rearrange("(g p j) d -> g p (j d)", p=P, j=4)
+        dx_hbm = out_0.rearrange("(g p j) d -> g j p d", p=P, j=4)
+
+        g_sb, w_sb, x_sb = {}, {}, {}
+
+        def load_grad(n):
+            g, fq = divmod(n, 4)
+            g_sb[n] = sbuf([P, 4 * PASS], BF16, "grad", 5)
+            cols = slice(PASS * (fq % 2), PASS * (fq % 2 + 1))
+            nc.sync.dma_start(out=g_sb[n][:].rearrange("p (j f) -> p j f", j=4), in_=grads[fq // 2][g][:, :, cols])
+
+        def load_weight(fq):
+            w_sb[fq] = sbuf([P, 8 * PASS], BF16, "big", 4)
+            cols = slice(PASS * (fq % 2), PASS * (fq % 2 + 1))
+            nc.sync.dma_start(out=w_sb[fq][:].rearrange("p (k f) -> p k f", k=8), in_=weights[fq // 2][:, :, cols])
+
+        def load_x(g):
+            x_sb[g] = sbuf([P, 4 * D], BF16, "x", 2)
+            nc.sync.dma_start(out=x_sb[g][:], in_=x_hbm[g])
+
+        gain_rows = sbuf([P, P], BF16, "gain_rows")
+        nc.vector.memset(gain_rows[:], 0.0)
+        nc.scalar.dma_start(out=gain_rows[0:8, :], in_=norm_w.rearrange("(k n) -> k n", n=P))
+        r_sb = sbuf([P, 8], F32, "rstd")
+        nc.sync.dma_start(out=r_sb[:].rearrange("p (g j) -> p g j", j=4), in_=rstd.rearrange("(g p j) o -> p g (j o)", p=P, j=4))
+        load_x(0)
+        load_grad(0)
+        load_weight(0)
+        load_grad(1)
+        load_weight(1)
+        load_grad(2)
+        load_weight(2)
+        load_x(1)
+        load_grad(3)
+        load_weight(3)
+        load_grad(4)
+
+        ident = sbuf([P, P], F32, "ident")
+        make_identity(nc, ident[:])
+        pos = sbuf([P, S], F32, "stage", 6)
+        for g in range(2):
+            nc.gpsimd.iota(pos[:, PASS * g : PASS * (g + 1)], pattern=[[1, 4], [4, P]], base=PASS * g, channel_multiplier=0, allow_small_or_imprecise_dtypes=True)
+
+        one_zero = sbuf([P, 2], F32, "one_zero")
+        nc.vector.memset(one_zero[:, 0:1], 1.0)
+        nc.vector.memset(one_zero[:, 1:2], 0.0)
+        quarter = sbuf([P, 1], F32, "quarter")
+        nc.vector.memset(quarter[0:64, :], 0.25)
+        nc.vector.memset(quarter[64:128, :], 0.0)
+        freq_rows = sbuf([P, PAIRS, 2], F32, "freq_rows")
+        for col in range(PAIRS):
+            u, q = divmod(col, 32)
+            turns = 1.0 / ROPE_BASE ** (2 * (2 * q + u) / HD) / (2 * math.pi)
+            hi = math.floor(turns * 65536) / 65536
+            nc.vector.tensor_scalar(out=freq_rows[:, col, :], in0=one_zero[:], scalar1=hi, scalar2=turns - hi, op0=ALU.mult, op1=ALU.max)
+        pick = sbuf([P, PAIRS], F32, "pick")
+        nc.vector.tensor_tensor(out=pick[:], in0=ident[:, 0:PAIRS], in1=ident[:, PAIRS:P], op=ALU.add)
+        ident_bf = sbuf([P, P], BF16, "ident_bf")
+        nc.vector.tensor_copy(out=ident_bf[:], in_=ident[:])
+        phase = sbuf([P, 1], F32, "phase")
+        nc.vector.tensor_scalar(out=phase[:], in0=quarter[:], scalar1=2 * math.pi, scalar2=None, op0=ALU.mult)
+        picked = sbuf([P, PAIRS, 2], F32, "picked")
+        nc.vector.tensor_tensor(out=picked[:], in0=freq_rows[:], in1=pick[:].unsqueeze(2).broadcast_to([P, PAIRS, 2]), op=ALU.mult)
+        freq = sbuf([P, 1], F32, "freq")
+        nc.vector.tensor_reduce(out=freq[:], in_=picked[:].rearrange("p c l -> p (c l)"), op=ALU.add, axis=AX.X)
+        freq_parts = sbuf([P, 2], F32, "freq_parts")
+        nc.vector.tensor_reduce(out=freq_parts[:], in_=picked[:].rearrange("p c l -> p l c"), op=ALU.add, axis=AX.X)
+
+        whole = sbuf([P, S], I32, "stage", 6)
+        frac = sbuf([P, S], F32, "stage", 6)
+        table = sbuf([P, S], F32, "stage", 6)
+        halves = [slice(0, PASS), slice(PASS, S)]
+
+        def whole_turns(g):
+            nc.vector.tensor_scalar(out=whole[:, halves[g]], in0=pos[:, halves[g]], scalar1=freq[:], scalar2=quarter[:], op0=ALU.mult, op1=ALU.add)
+
+        def frac_high(g):
+            nc.vector.scalar_tensor_tensor(out=frac[:, halves[g]], in0=pos[:, halves[g]], scalar=freq_parts[:, 0:1], in1=whole[:, halves[g]], op0=ALU.mult, op1=ALU.subtract)
+
+        def frac_low(g):
+            nc.vector.scalar_tensor_tensor(out=frac[:, halves[g]], in0=pos[:, halves[g]], scalar=freq_parts[:, 1:2], in1=frac[:, halves[g]], op0=ALU.mult, op1=ALU.add)
+            nc.scalar.activation(out=table[:, halves[g]], in_=frac[:, halves[g]], func=ACT.Sin, scale=2 * math.pi, bias=phase[:])
+
+        tab = {}
+
+        def table_to_psum(g, b):
+            tab[g] = bank(b)
+            for j in range(4):
+                nc.tensor.transpose(tab[g][:, P * j : P * (j + 1)], table[:, PASS * g + P * j : PASS * g + P * (j + 1)], ident[:])
+
+        gain_ps = bank(2, BF16)
+        for k in range(8):
+            nc.tensor.matmul(out=gain_ps[:, P * k : P * (k + 1)], lhsT=ident_bf[:, k : k + 1].to_broadcast([P, P]), rhs=gain_rows[:], start=True, stop=True)
+        gain_t = bank(7, BF16)
+        nc.tensor.transpose(gain_t[:, 0:P], gain_rows[:], ident_bf[:])
+
+        neg_r2 = sbuf([P, 8], F32, "neg_r2")
+        whole_turns(0)
+        whole_turns(1)
+        frac_high(0)
+        nc.vector.scalar_tensor_tensor(out=neg_r2[:], in0=r_sb[:], scalar=-1.0 / D, in1=r_sb[:], op0=ALU.mult, op1=ALU.mult)
+        frac_low(0)
+        table_to_psum(0, 0)
+        frac_high(1)
+        gain_col = sbuf([P, 8], F32, "gain_col")
+        nc.scalar.copy(out=gain_col[:], in_=gain_t[:, 0:8])
+
+        h_raw, h_mix, h_q = {}, {}, {}
+
+        def h_slot(g, j):
+            if j == 0:
+                h_raw[g] = sbuf([P, 4 * D], BF16, "h_raw", 2)
+            cols = slice(D * j, D * (j + 1))
+            nc.vector.scalar_tensor_tensor(out=h_raw[g][:, cols], in0=x_sb[g][:, cols], scalar=r_sb[:, 4 * g + j : 4 * g + j + 1], in1=gain_ps[:], op0=ALU.mult, op1=ALU.mult)
+
+        def h_interleave(g, half):
+            h_mix[g, half] = sbuf([P, 4 * PASS], BF16, "h_mix", 3)
+            src = h_raw[g][:].rearrange("p (j a c i) -> p a c j i", j=4, a=2, i=4)[:, half]
+            nc.scalar.copy(out=h_mix[g, half][:].rearrange("p (c i j) -> p c j i", i=4, j=4), in_=src)
+
+        def quantize(src, fmt, tag, bufs):
+            codes = sbuf([P, PASS], U32, tag + "_codes", bufs)
+            scales = sbuf([P, PASS], U8, tag + "_scales", bufs)
+            nc.vector.quantize_mx(out=codes[:].bitcast(fmt), scales=scales[:], in_=src[:])
+            return codes, scales
+
+        def h_quantize(g, half):
+            h_q[g, half] = quantize(h_mix[g, half], E4M3, "h", 4)
+
+        w_mix, w_q = {}, {}
+
+        def w_transpose(fq, half, banks):
+            w_mix[fq, half] = sbuf([P, 4 * PASS], BF16, "w_mix", 2)
+            words = w_sb[fq][:].bitcast(F32)
+            mixed = w_mix[fq, half][:].bitcast(F32).rearrange("p (b k d u) -> p b k d u", b=2, k=2, u=2)
+            for b in range(2):
+                turned = bank(banks[b])
+                for kk in range(2):
+                    k = 4 * half + 2 * b + kk
+                    for u in range(2):
+                        at = P * (2 * kk + u)
+                        nc.tensor.transpose(turned[:, at : at + P], words[:, 256 * k + u : 256 * (k + 1) : 2], ident[:])
+                nc.scalar.copy(out=mixed[:, b], in_=turned[:].rearrange("p (k u d) -> p k d u", k=2, u=2))
+
+        def w_quantize(fq, half):
+            w_q[fq, half] = quantize(w_mix[fq, half], E4M3, "w", 8)
+
+        prod, dz_tok, dz_feat, dz_tok_q, dz_feat_q = {}, {}, {}, {}, {}
+
+        def rope_product(n, t, heads=slice(0, 4)):
+            if heads.start == 0:
+                prod[n, t] = sbuf([P, 2 * PASS], F32, "prod", 5)
+            shape = [P, 4, 2, heads.stop - heads.start, 32]
+            src = g_sb[n][:].rearrange("p (j h q t) -> p t j h q", j=4, h=4, t=4)[:, t, :, heads]
+            factor = tab[n // 4][:].rearrange("p (j l u q) -> p u j l q", j=4, l=2, u=2)[:, t // 2]
+            out = prod[n, t][:].rearrange("p (j l h q) -> p j l h q", j=4, l=2, h=4)[:, :, :, heads]
+            nc.vector.tensor_tensor(out=out, in0=src.unsqueeze(2).broadcast_to(shape), in1=factor.unsqueeze(3).broadcast_to(shape), op=ALU.mult)
+
+        def rope_sum(n, u, engine):
+            if u == 0:
+                dz_tok[n] = sbuf([P, 4 * PASS], BF16, "dz_tok", 3)
+            even = prod[n, 2 * u][:].rearrange("p (j l c i) -> p l c j i", j=4, l=2, i=4)
+            odd = prod[n, 2 * u + 1][:].rearrange("p (j l c i) -> p l c j i", j=4, l=2, i=4)
+            out = dz_tok[n][:].rearrange("p (t c i j) -> p t c j i", t=4, i=4, j=4)
+            engine.tensor_tensor(out=out[:, 2 * u], in0=even[:, 0], in1=odd[:, 1], op=ALU.add)
+            engine.tensor_tensor(out=out[:, 2 * u + 1], in0=odd[:, 0], in1=even[:, 1], op=ALU.subtract)
+
+        def dz_transpose(n, banks):
+            dz_feat[n] = sbuf([P, 4 * PASS], BF16, "dz_feat", 2)
+            words = dz_tok[n][:].bitcast(F32)
+            for jp in range(2):
+                turned = bank(banks[jp])
+                for t in range(4):
+                    nc.tensor.transpose(turned[:, P * t : P * (t + 1)], words[:, 256 * t + jp : 256 * (t + 1) : 2], ident[:])
+                out = dz_feat[n][:].rearrange("r (a e p t) -> r a e p t", a=2, e=2, t=4)[:, jp]
+                nc.scalar.copy(out=out, in_=turned[:].bitcast(BF16).rearrange("r (t p e) -> r e p t", t=4, e=2))
+
+        def tok_quantize(n):
+            dz_tok_q[n] = quantize(dz_tok[n], E5M2, "dz_tok", 6)
+
+        def feat_quantize(n):
+            dz_feat_q[n] = quantize(dz_feat[n], E5M2, "dz_feat", 6)
+
+        t_feat = {}
+
+        dh_acc = {}
+
+        def dh_passes(g, k, b, passes):
+            if passes[0] == 0:
+                dh_acc[g, k] = bank(b)
+            acc = dh_acc[g, k]
+            cols = slice(P * (k % 4), P * (k % 4 + 1))
+            for fq in passes:
+                w_codes, w_scales = w_q[fq, k // 4]
+                z_codes, z_scales = dz_feat_q[4 * g + fq]
+                nc.tensor.matmul_mx(out=acc[:], lhsT=w_codes[:, cols].bitcast(E4M3), lhsT_scale=w_scales[:, cols],
+                                    rhs=z_codes[:].bitcast(E5M2), rhs_scale=z_scales[:], start=(fq == 0), stop=(fq == 3))
+            if passes[-1] < 3:
+                return
+            if k % 4 == 0:
+                t_feat[g, k // 4] = sbuf([P, 4 * PASS], F32, "big", 4)
+            nc.scalar.activation(out=t_feat[g, k // 4][:, PASS * (k % 4) : PASS * (k % 4 + 1)], in_=acc[:], func=ACT.Copy, scale=gain_col[:, k : k + 1])
+
+        dw_stage = {}
+
+        def dw_block(fq, k, b):
+            if k % 2 == 0:
+                dw_stage[fq, k // 2] = sbuf([P, 2 * PASS], F32, "stage", 6)
+            stage = dw_stage[fq, k // 2]
+            acc = bank(b)
+            cols = slice(P * (k % 4), P * (k % 4 + 1))
+            for g in range(2):
+                h_codes, h_scales = h_q[g, k // 4]
+                z_codes, z_scales = dz_tok_q[4 * g + fq]
+                nc.tensor.matmul_mx(out=acc[:], lhsT=h_codes[:, cols].bitcast(E4M3), lhsT_scale=h_scales[:, cols],
+                                    rhs=z_codes[:].bitcast(E5M2), rhs_scale=z_scales[:], start=(g == 0), stop=(g == 1))
+            out = stage[:, PASS * (k % 2) : PASS * (k % 2 + 1)].rearrange("p (r t) -> p r t", t=4)
+            nc.scalar.copy(out=out, in_=acc[:].rearrange("p (t r) -> p r t", t=4))
+            if k % 2 == 1:
+                feats = slice(PASS * (fq % 2), PASS * (fq % 2 + 1))
+                nc.sync.dma_start(out=dws[fq // 2][:, k - 1 : k + 1, feats], in_=stage[:].rearrange("p (k f) -> p k f", k=2))
+
+        t_tok, dx = {}, {}
+
+        def t_transpose(g, j, half, b):
+            t_tok[g, j, half] = bank(b)
+            for kk in range(4):
+                at = PASS * kk + P * j
+                nc.tensor.transpose(t_tok[g, j, half][:, P * kk : P * (kk + 1)], t_feat[g, half][:, at : at + P], ident[:])
+
+        sums = {}
+
+        def norm_mean(g, j, half):
+            slot = slice(4 * g + j, 4 * g + j + 1)
+            if half == 0:
+                dx[g, j] = sbuf([P, D], F32, "grad", 5)
+                sums[g, j] = sbuf([P, 2], F32, "sums", 4)
+            nc.vector.scalar_tensor_tensor(out=dx[g, j][:, halves[half]], in0=t_tok[g, j, half][:], scalar=r_sb[:, slot],
+                                           in1=x_sb[g][:, D * j + PASS * half : D * j + PASS * (half + 1)],
+                                           op0=ALU.mult, op1=ALU.mult, accum_out=sums[g, j][:, half : half + 1])
+            if half == 1:
+                coef = sbuf([P, 1], F32, "coef", 2)
+                nc.gpsimd.tensor_scalar(out=coef[:], in0=sums[g, j][:, 0:1], scalar1=sums[g, j][:, 1:2], scalar2=neg_r2[:, slot], op0=ALU.add, op1=ALU.mult)
+                nc.gpsimd.tensor_scalar(out=dx[g, j][:], in0=x_sb[g][:, D * j : D * (j + 1)], scalar1=coef[:], scalar2=0.0, op0=ALU.mult, op1=ALU.add)
+
+        def norm_finish(g, j):
+            slot = slice(4 * g + j, 4 * g + j + 1)
+            for half in range(2):
+                part = dx[g, j][:, halves[half]]
+                nc.vector.scalar_tensor_tensor(out=part, in0=t_tok[g, j, half][:], scalar=r_sb[:, slot], in1=part, op0=ALU.mult, op1=ALU.add)
+            nc.sync.dma_start(out=dx_hbm[g, j], in_=dx[g, j][:])
+
+        def open_chunk(n):
+            rope_product(n, 0)
+            rope_product(n, 1)
+            rope_sum(n, 0, nc.gpsimd)
+            rope_product(n, 2)
+            rope_product(n, 3, slice(0, 3))
+
+        def close_chunk(n, engine):
+            rope_product(n, 3, slice(3, 4))
+            rope_sum(n, 1, engine)
+            if n + 5 < 8:
+                load_grad(n + 5)
+
+        every_pass = range(4)
+
+        def tile_mean(g, j, banks):
+            for half in range(2):
+                t_transpose(g, j, half, banks[half])
+            for half in range(2):
+                norm_mean(g, j, half)
+
+        frac_low(1)
+        w_transpose(0, 0, (3, 4))
+        w_transpose(0, 1, (5, 6))
+        for n in range(4):
+            open_chunk(n)
+            h_slot(0, n)
+            if n > 0:
+                dz_transpose(n - 1, (3, 4))
+                tok_quantize(n - 1)
+            w_quantize(n, 0)
+            w_quantize(n, 1)
+            if n < 3:
+                w_transpose(n + 1, 0, (5, 1))
+                w_transpose(n + 1, 1, (3, 4))
+            if n > 1:
+                feat_quantize(n - 2)
+                for k in range(2):
+                    dh_passes(0, k, (6, 7)[k], [n - 2])
+            if n == 3:
+                table_to_psum(1, 1)
+                h_slot(1, 0)
+            close_chunk(n, nc.gpsimd)
+        h_interleave(0, 0)
+        open_chunk(4)
+        h_slot(1, 1)
+        dz_transpose(3, (3, 4))
+        h_interleave(0, 1)
+        feat_quantize(2)
+        tok_quantize(3)
+        h_quantize(0, 0)
+        for k in range(2):
+            dh_passes(0, k, None, [2])
+        for k in range(2, 4):
+            dh_passes(0, k, (5, 0)[k - 2], range(3))
+        feat_quantize(3)
+        close_chunk(4, nc.gpsimd)
+        for k in range(4):
+            dh_passes(0, k, None, [3])
+        h_slot(1, 2)
+        h_slot(1, 3)
+        open_chunk(5)
+        dh_passes(0, 4, 6, every_pass)
+        h_interleave(1, 0)
+        dz_transpose(4, (3, 4))
+        for k in range(5, 8):
+            dh_passes(0, k, (7, 5, 0)[k - 5], every_pass)
+        tok_quantize(4)
+        h_quantize(0, 1)
+        h_quantize(1, 0)
+        h_interleave(1, 1)
+        close_chunk(5, nc.gpsimd)
+        mx_banks = (5, 6, 0)
+        tile_mean(0, 0, (7, 2))
+        for k in range(4):
+            dw_block(0, k, mx_banks[k % 3])
+        open_chunk(6)
+        dz_transpose(5, (3, 4))
+        norm_finish(0, 0)
+        h_quantize(1, 1)
+        feat_quantize(4)
+        tok_quantize(5)
+        close_chunk(6, nc.gpsimd)
+        tile_mean(0, 1, (7, 2))
+        for k in range(4, 8):
+            dw_block(0, k, mx_banks[k % 3])
+        for k in range(4):
+            dw_block(1, k, mx_banks[(k + 2) % 3])
+        open_chunk(7)
+        dz_transpose(6, (3, 4))
+        norm_finish(0, 1)
+        feat_quantize(5)
+        tok_quantize(6)
+        close_chunk(7, nc.vector)
+        for k in range(4, 8):
+            dw_block(1, k, mx_banks[(k + 2) % 3])
+        tok_quantize(7)
+        feat_quantize(6)
+        dz_transpose(7, (3, 4))
+        tile_mean(0, 2, (7, 2))
+        for k in range(4):
+            dw_block(2, k, (1, 5)[k % 2])
+        feat_quantize(7)
+        for k in range(2):
+            dh_passes(1, k, (6, 0)[k], range(3))
+        norm_finish(0, 2)
+        for k in range(2):
+            dh_passes(1, k, None, [3])
+        tile_mean(0, 3, (7, 2))
+        for k in range(2, 4):
+            dh_passes(1, k, (3, 4)[k % 2], every_pass)
+        norm_finish(0, 3)
+        for j in range(3):
+            dh_passes(1, 4 + j, (6, 0)[j % 2], every_pass)
+            t_transpose(1, j, 0, (1, 5, 3)[j])
+            norm_mean(1, j, 0)
+        dh_passes(1, 7, 0, every_pass)
+        rest = [(2, k) for k in range(4, 8)] + [(3, k) for k in range(8)]
+        dw_block(2, 4, 6)
+        for j in range(3):
+            t_transpose(1, j, 1, (4, 7, 2)[j])
+            norm_mean(1, j, 1)
+        for i in range(1, 4):
+            dw_block(rest[i][0], rest[i][1], (6, 0)[i % 2])
+        norm_finish(1, 0)
+        tile_mean(1, 3, (1, 4))
+        norm_finish(1, 1)
+        for i in range(4, 12):
+            dw_block(rest[i][0], rest[i][1], (6, 0)[i % 2])
+        norm_finish(1, 2)
+        norm_finish(1, 3)

@@ -23,6 +23,8 @@ AX = mybir.AxisListType
 P = 128
 PASS = 512
 PAIRS = HD // 2
+VECTOR_COLUMNS = 30
+ON_VECTOR = (3, 4)
 
 
 def tile_attentionmodule_pa_v_kernel(tc, xs, norm_w, wq, wk, rstd, grad_0, grad_1, out_0, out_1, out_2):
@@ -54,7 +56,7 @@ def tile_attentionmodule_pa_v_kernel(tc, xs, norm_w, wq, wk, rstd, grad_0, grad_
             nc.sync.dma_start(out=g_sb[n][:].rearrange("p (j f) -> p j f", j=4), in_=grads[fq // 2][g][:, :, cols])
 
         def load_weight(fq):
-            w_sb[fq] = sbuf([P, 8 * PASS], BF16, "big", 4)
+            w_sb[fq] = sbuf([P, 8 * PASS], BF16, "big", 3)
             cols = slice(PASS * (fq % 2), PASS * (fq % 2 + 1))
             nc.sync.dma_start(out=w_sb[fq][:].rearrange("p (k f) -> p k f", k=8), in_=weights[fq // 2][:, :, cols])
 
@@ -67,23 +69,21 @@ def tile_attentionmodule_pa_v_kernel(tc, xs, norm_w, wq, wk, rstd, grad_0, grad_
         nc.scalar.dma_start(out=gain_rows[0:8, :], in_=norm_w.rearrange("(k n) -> k n", n=P))
         r_sb = sbuf([P, 8], F32, "rstd")
         nc.sync.dma_start(out=r_sb[:].rearrange("p (g j) -> p g j", j=4), in_=rstd.rearrange("(g p j) o -> p g (j o)", p=P, j=4))
-        load_x(0)
         load_grad(0)
         load_weight(0)
+        load_x(0)
         load_grad(1)
         load_weight(1)
         load_grad(2)
         load_weight(2)
         load_x(1)
         load_grad(3)
-        load_weight(3)
         load_grad(4)
 
         ident = sbuf([P, P], F32, "ident")
         make_identity(nc, ident[:])
         pos = sbuf([P, S], F32, "stage", 6)
-        for g in range(2):
-            nc.gpsimd.iota(pos[:, PASS * g : PASS * (g + 1)], pattern=[[1, 4], [4, P]], base=PASS * g, channel_multiplier=0, allow_small_or_imprecise_dtypes=True)
+        nc.gpsimd.iota(pos[:, 0:PASS], pattern=[[1, 4], [4, P]], base=0, channel_multiplier=0, allow_small_or_imprecise_dtypes=True)
 
         one_zero = sbuf([P, 2], F32, "one_zero")
         nc.vector.memset(one_zero[:, 0:1], 1.0)
@@ -96,7 +96,12 @@ def tile_attentionmodule_pa_v_kernel(tc, xs, norm_w, wq, wk, rstd, grad_0, grad_
             u, q = divmod(col, 32)
             turns = 1.0 / ROPE_BASE ** (2 * (2 * q + u) / HD) / (2 * math.pi)
             hi = math.floor(turns * 65536) / 65536
-            nc.vector.tensor_scalar(out=freq_rows[:, col, :], in0=one_zero[:], scalar1=hi, scalar2=turns - hi, op0=ALU.mult, op1=ALU.max)
+            lo = turns - hi
+            if col < VECTOR_COLUMNS:
+                nc.vector.tensor_scalar(out=freq_rows[:, col, :], in0=one_zero[:], scalar1=hi - lo, scalar2=lo, op0=ALU.mult, op1=ALU.add)
+            else:
+                nc.scalar.activation(out=freq_rows[:, col, :], in_=one_zero[:], func=ACT.Copy, scale=hi - lo, bias=lo)
+        nc.scalar.activation(out=pos[:, PASS:S], in_=pos[:, 0:PASS], func=ACT.Copy, bias=float(PASS))
         pick = sbuf([P, PAIRS], F32, "pick")
         nc.vector.tensor_tensor(out=pick[:], in0=ident[:, 0:PAIRS], in1=ident[:, PAIRS:P], op=ALU.add)
         ident_bf = sbuf([P, P], BF16, "ident_bf")
@@ -132,13 +137,8 @@ def tile_attentionmodule_pa_v_kernel(tc, xs, norm_w, wq, wk, rstd, grad_0, grad_
             for j in range(4):
                 nc.tensor.transpose(tab[g][:, P * j : P * (j + 1)], table[:, PASS * g + P * j : PASS * g + P * (j + 1)], ident[:])
 
-        gain_ps = bank(2, BF16)
-        for k in range(8):
-            nc.tensor.matmul(out=gain_ps[:, P * k : P * (k + 1)], lhsT=ident_bf[:, k : k + 1].to_broadcast([P, P]), rhs=gain_rows[:], start=True, stop=True)
-        gain_t = bank(7, BF16)
-        nc.tensor.transpose(gain_t[:, 0:P], gain_rows[:], ident_bf[:])
-
         neg_r2 = sbuf([P, 8], F32, "neg_r2")
+        neg_r3 = sbuf([P, 8], F32, "neg_r3")
         whole_turns(0)
         whole_turns(1)
         frac_high(0)
@@ -146,14 +146,14 @@ def tile_attentionmodule_pa_v_kernel(tc, xs, norm_w, wq, wk, rstd, grad_0, grad_
         frac_low(0)
         table_to_psum(0, 0)
         frac_high(1)
+        nc.vector.tensor_tensor(out=neg_r3[:], in0=neg_r2[:], in1=r_sb[:], op=ALU.mult)
         gain_col = sbuf([P, 8], F32, "gain_col")
-        nc.scalar.copy(out=gain_col[:], in_=gain_t[:, 0:8])
 
         h_raw, h_mix, h_q = {}, {}, {}
 
         def h_slot(g, j):
             if j == 0:
-                h_raw[g] = sbuf([P, 4 * D], BF16, "h_raw", 2)
+                h_raw[g] = sbuf([P, 4 * D], (BF16, F32)[g], "h_raw%d" % g)
             cols = slice(D * j, D * (j + 1))
             nc.vector.scalar_tensor_tensor(out=h_raw[g][:, cols], in0=x_sb[g][:, cols], scalar=r_sb[:, 4 * g + j : 4 * g + j + 1], in1=gain_ps[:], op0=ALU.mult, op1=ALU.mult)
 
@@ -209,7 +209,7 @@ def tile_attentionmodule_pa_v_kernel(tc, xs, norm_w, wq, wk, rstd, grad_0, grad_
             engine.tensor_tensor(out=out[:, 2 * u], in0=even[:, 0], in1=odd[:, 1], op=ALU.add)
             engine.tensor_tensor(out=out[:, 2 * u + 1], in0=odd[:, 0], in1=even[:, 1], op=ALU.subtract)
 
-        def dz_transpose(n, banks):
+        def dz_transpose(n, banks, copies=(nc.scalar.copy, nc.scalar.copy)):
             dz_feat[n] = sbuf([P, 4 * PASS], BF16, "dz_feat", 2)
             words = dz_tok[n][:].bitcast(F32)
             for jp in range(2):
@@ -217,7 +217,7 @@ def tile_attentionmodule_pa_v_kernel(tc, xs, norm_w, wq, wk, rstd, grad_0, grad_
                 for t in range(4):
                     nc.tensor.transpose(turned[:, P * t : P * (t + 1)], words[:, 256 * t + jp : 256 * (t + 1) : 2], ident[:])
                 out = dz_feat[n][:].rearrange("r (a e p t) -> r a e p t", a=2, e=2, t=4)[:, jp]
-                nc.scalar.copy(out=out, in_=turned[:].bitcast(BF16).rearrange("r (t p e) -> r e p t", t=4, e=2))
+                copies[jp](out=out, in_=turned[:].bitcast(BF16).rearrange("r (t p e) -> r e p t", t=4, e=2))
 
         def tok_quantize(n):
             dz_tok_q[n] = quantize(dz_tok[n], E5M2, "dz_tok", 6)
@@ -242,8 +242,12 @@ def tile_attentionmodule_pa_v_kernel(tc, xs, norm_w, wq, wk, rstd, grad_0, grad_
             if passes[-1] < 3:
                 return
             if k % 4 == 0:
-                t_feat[g, k // 4] = sbuf([P, 4 * PASS], F32, "big", 4)
-            nc.scalar.activation(out=t_feat[g, k // 4][:, PASS * (k % 4) : PASS * (k % 4 + 1)], in_=acc[:], func=ACT.Copy, scale=gain_col[:, k : k + 1])
+                t_feat[g, k // 4] = sbuf([P, 4 * PASS], F32, "big", 3)
+            out = t_feat[g, k // 4][:, PASS * (k % 4) : PASS * (k % 4 + 1)]
+            if k in ON_VECTOR:
+                nc.vector.tensor_scalar(out=out, in0=acc[:], scalar1=gain_col[:, k : k + 1], scalar2=None, op0=ALU.mult)
+            else:
+                nc.scalar.activation(out=out, in_=acc[:], func=ACT.Copy, scale=gain_col[:, k : k + 1])
 
         dw_stage = {}
 
@@ -279,13 +283,59 @@ def tile_attentionmodule_pa_v_kernel(tc, xs, norm_w, wq, wk, rstd, grad_0, grad_
             if half == 0:
                 dx[g, j] = sbuf([P, D], F32, "grad", 5)
                 sums[g, j] = sbuf([P, 2], F32, "sums", 4)
-            nc.vector.scalar_tensor_tensor(out=dx[g, j][:, halves[half]], in0=t_tok[g, j, half][:], scalar=r_sb[:, slot],
+            nc.vector.scalar_tensor_tensor(out=dx[g, j][:, halves[half]], in0=t_tok[g, j, half][:], scalar=neg_r3[:, slot],
                                            in1=x_sb[g][:, D * j + PASS * half : D * j + PASS * (half + 1)],
                                            op0=ALU.mult, op1=ALU.mult, accum_out=sums[g, j][:, half : half + 1])
-            if half == 1:
-                coef = sbuf([P, 1], F32, "coef", 2)
-                nc.gpsimd.tensor_scalar(out=coef[:], in0=sums[g, j][:, 0:1], scalar1=sums[g, j][:, 1:2], scalar2=neg_r2[:, slot], op0=ALU.add, op1=ALU.mult)
-                nc.gpsimd.tensor_scalar(out=dx[g, j][:], in0=x_sb[g][:, D * j : D * (j + 1)], scalar1=coef[:], scalar2=0.0, op0=ALU.mult, op1=ALU.add)
+
+        def norm_shift(g, j):
+            coef = sbuf([P, 1], F32, "coef", 2)
+            nc.vector.tensor_reduce(out=coef[:], in_=sums[g, j][:], op=ALU.add, axis=AX.X)
+            nc.gpsimd.tensor_scalar(out=dx[g, j][:], in0=x_sb[g][:, D * j : D * (j + 1)], scalar1=coef[:], scalar2=0.0, op0=ALU.mult, op1=ALU.add)
+
+        dh_tok = {}
+
+        def dh_tile_passes(j, banks, passes):
+            for half in range(2):
+                if passes[0] == 0:
+                    dh_tok[j, half] = bank(banks[half])
+                for fq in passes:
+                    w_codes, w_scales = w_q[fq, half]
+                    z_codes, z_scales = dz_feat_q[4 + fq]
+                    cols = slice(P * j, P * (j + 1))
+                    nc.tensor.matmul_mx(out=dh_tok[j, half][:], lhsT=z_codes[:, cols].bitcast(E5M2), lhsT_scale=z_scales[:, cols],
+                                        rhs=w_codes[:].bitcast(E4M3), rhs_scale=w_scales[:], start=(fq == 0), stop=(fq == 3))
+
+        shift, coefs = {}, {}
+
+        def tile_mean(j):
+            shift[j] = sbuf([P, D], F32, "prod", 5)
+            sums[1, j] = sbuf([P, 2], F32, "sums", 4)
+            for half in range(2):
+                nc.vector.scalar_tensor_tensor(out=shift[j][:, halves[half]], in0=dh_tok[j, half][:], scalar=neg_r2[:, 4 + j : 5 + j],
+                                               in1=h_raw[1][:, D * j + PASS * half : D * j + PASS * (half + 1)],
+                                               op0=ALU.mult, op1=ALU.mult, accum_out=sums[1, j][:, half : half + 1])
+
+        def tile_gain(j):
+            dx[1, j] = sbuf([P, D], F32, "grad", 5)
+            coefs[j] = sbuf([P, 1], F32, "coef", 2)
+            for half in range(2):
+                nc.vector.scalar_tensor_tensor(out=dx[1, j][:, halves[half]], in0=dh_tok[j, half][:], scalar=r_sb[:, 4 + j : 5 + j],
+                                               in1=gain_wide[:, halves[half]], op0=ALU.mult, op1=ALU.mult)
+                if half == 0:
+                    nc.vector.tensor_reduce(out=coefs[j][:], in_=sums[1, j][:], op=ALU.add, axis=AX.X)
+
+        def tile_finish(j):
+            nc.scalar.activation(out=shift[j][:], in_=x_sb[1][:, D * j : D * (j + 1)], func=ACT.Copy, scale=coefs[j][:])
+            for half in range(2):
+                part = dx[1, j][:, halves[half]]
+                nc.gpsimd.tensor_tensor(out=part, in0=part, in1=shift[j][:, halves[half]], op=ALU.add)
+                nc.sync.dma_start(out=dx_hbm[1, j][:, halves[half]], in_=part)
+
+        def last_tile_finish(j):
+            for half in range(2):
+                part = dx[1, j][:, halves[half]]
+                nc.vector.scalar_tensor_tensor(out=part, in0=x_sb[1][:, D * j + PASS * half : D * j + PASS * (half + 1)], scalar=coefs[j][:], in1=part, op0=ALU.mult, op1=ALU.add)
+                nc.sync.dma_start(out=dx_hbm[1, j][:, halves[half]], in_=part)
 
         def norm_finish(g, j):
             slot = slice(4 * g + j, 4 * g + j + 1)
@@ -294,10 +344,12 @@ def tile_attentionmodule_pa_v_kernel(tc, xs, norm_w, wq, wk, rstd, grad_0, grad_
                 nc.vector.scalar_tensor_tensor(out=part, in0=t_tok[g, j, half][:], scalar=r_sb[:, slot], in1=part, op0=ALU.mult, op1=ALU.add)
             nc.sync.dma_start(out=dx_hbm[g, j], in_=dx[g, j][:])
 
-        def open_chunk(n):
+        def first_products(n):
             rope_product(n, 0)
             rope_product(n, 1)
             rope_sum(n, 0, nc.gpsimd)
+
+        def second_products(n):
             rope_product(n, 2)
             rope_product(n, 3, slice(0, 3))
 
@@ -307,20 +359,35 @@ def tile_attentionmodule_pa_v_kernel(tc, xs, norm_w, wq, wk, rstd, grad_0, grad_
             if n + 5 < 8:
                 load_grad(n + 5)
 
-        every_pass = range(4)
+        def t_banks_fill(j):
+            for half in range(2):
+                t_transpose(0, j, half, (7, 2)[half])
 
-        def tile_mean(g, j, banks):
+        def mean_terms(j):
             for half in range(2):
-                t_transpose(g, j, half, banks[half])
-            for half in range(2):
-                norm_mean(g, j, half)
+                norm_mean(0, j, half)
+
+        every_pass = range(4)
+        mx_banks = (5, 6, 0)
 
         frac_low(1)
+        gain_ps = bank(2, BF16)
+        for k in range(8):
+            nc.tensor.matmul(out=gain_ps[:, P * k : P * (k + 1)], lhsT=ident_bf[:, k : k + 1].to_broadcast([P, P]), rhs=gain_rows[:], start=True, stop=True)
+        gain_t = bank(7, BF16)
+        nc.tensor.transpose(gain_t[:, 0:P], gain_rows[:], ident_bf[:])
+
         w_transpose(0, 0, (3, 4))
         w_transpose(0, 1, (5, 6))
+        nc.scalar.copy(out=gain_col[:], in_=gain_t[:, 0:8])
+        load_weight(3)
+        h_first = ((0, 0), (0, 2), (1, 0), (1, 1))
         for n in range(4):
-            open_chunk(n)
-            h_slot(0, n)
+            if n == 2:
+                h_interleave(0, 0)
+            first_products(n)
+            second_products(n)
+            h_slot(*h_first[n])
             if n > 0:
                 dz_transpose(n - 1, (3, 4))
                 tok_quantize(n - 1)
@@ -329,99 +396,120 @@ def tile_attentionmodule_pa_v_kernel(tc, xs, norm_w, wq, wk, rstd, grad_0, grad_
             if n < 3:
                 w_transpose(n + 1, 0, (5, 1))
                 w_transpose(n + 1, 1, (3, 4))
-            if n > 1:
-                feat_quantize(n - 2)
-                for k in range(2):
-                    dh_passes(0, k, (6, 7)[k], [n - 2])
+            if n == 2:
+                gain_wide = sbuf([P, D], BF16, "gain_wide")
+                nc.scalar.copy(out=gain_wide[:], in_=gain_ps[:])
             if n == 3:
                 table_to_psum(1, 1)
-                h_slot(1, 0)
+                h_interleave(0, 1)
+                dh_passes(0, 2, 5, range(2))
             close_chunk(n, nc.gpsimd)
-        h_interleave(0, 0)
-        open_chunk(4)
-        h_slot(1, 1)
-        dz_transpose(3, (3, 4))
-        h_interleave(0, 1)
-        feat_quantize(2)
-        tok_quantize(3)
-        h_quantize(0, 0)
-        for k in range(2):
-            dh_passes(0, k, None, [2])
-        for k in range(2, 4):
-            dh_passes(0, k, (5, 0)[k - 2], range(3))
-        feat_quantize(3)
-        close_chunk(4, nc.gpsimd)
-        for k in range(4):
-            dh_passes(0, k, None, [3])
+            if n > 0:
+                feat_quantize(n - 1)
+                for k in range(2 if n < 3 else 3):
+                    dh_passes(0, k, (6, 7, 5)[k], [n - 1])
+            if n < 2:
+                h_slot(0, 2 * n + 1)
+        first_products(4)
         h_slot(1, 2)
         h_slot(1, 3)
-        open_chunk(5)
-        dh_passes(0, 4, 6, every_pass)
+        dh_passes(0, 3, 0, range(3))
+        dz_transpose(3, (3, 4))
+        dh_passes(0, 4, 2, range(3))
         h_interleave(1, 0)
-        dz_transpose(4, (3, 4))
-        for k in range(5, 8):
-            dh_passes(0, k, (7, 5, 0)[k - 5], every_pass)
-        tok_quantize(4)
+        second_products(4)
+        tok_quantize(3)
+        h_quantize(0, 0)
         h_quantize(0, 1)
-        h_quantize(1, 0)
+        close_chunk(4, nc.gpsimd)
+        feat_quantize(3)
+        for k in range(3):
+            dh_passes(0, k, None, [3])
         h_interleave(1, 1)
-        close_chunk(5, nc.gpsimd)
-        mx_banks = (5, 6, 0)
-        tile_mean(0, 0, (7, 2))
-        for k in range(4):
-            dw_block(0, k, mx_banks[k % 3])
-        open_chunk(6)
-        dz_transpose(5, (3, 4))
-        norm_finish(0, 0)
+        first_products(5)
+        for k in range(3, 5):
+            dh_passes(0, k, None, [3])
+        dh_passes(0, 5, 6, every_pass)
+        dz_transpose(4, (3, 4))
+        for k in range(6, 8):
+            dh_passes(0, k, (5, 0)[k - 6], every_pass)
+        t_banks_fill(0)
+        second_products(5)
+        tok_quantize(4)
+        h_quantize(1, 0)
         h_quantize(1, 1)
+        close_chunk(5, nc.gpsimd)
+        for k in range(4):
+            dw_block(0, k, mx_banks[(k + 1) % 3])
+        rope_product(6, 0)
+        mean_terms(0)
+        rope_product(6, 1)
+        norm_shift(0, 0)
+        rope_sum(6, 0, nc.gpsimd)
+        dz_transpose(5, (3, 4))
+        for k in range(4, 8):
+            dw_block(0, k, mx_banks[(k + 1) % 3])
+        second_products(6)
+        norm_finish(0, 0)
+        t_banks_fill(1)
         feat_quantize(4)
         tok_quantize(5)
         close_chunk(6, nc.gpsimd)
-        tile_mean(0, 1, (7, 2))
-        for k in range(4, 8):
-            dw_block(0, k, mx_banks[k % 3])
-        for k in range(4):
-            dw_block(1, k, mx_banks[(k + 2) % 3])
-        open_chunk(7)
-        dz_transpose(6, (3, 4))
-        norm_finish(0, 1)
         feat_quantize(5)
-        tok_quantize(6)
-        close_chunk(7, nc.vector)
-        for k in range(4, 8):
-            dw_block(1, k, mx_banks[(k + 2) % 3])
-        tok_quantize(7)
-        feat_quantize(6)
-        dz_transpose(7, (3, 4))
-        tile_mean(0, 2, (7, 2))
         for k in range(4):
-            dw_block(2, k, (1, 5)[k % 2])
+            dw_block(1, k, mx_banks[k % 3])
+        rope_product(7, 0)
+        mean_terms(1)
+        rope_product(7, 1, slice(0, 3))
+        norm_shift(0, 1)
+        dz_transpose(6, (3, 4))
+        for k in range(4, 8):
+            dw_block(1, k, mx_banks[k % 3])
+        rope_product(7, 2)
+        tok_quantize(6)
+        rope_product(7, 1, slice(3, 4))
+        rope_sum(7, 0, nc.gpsimd)
+        norm_finish(0, 1)
+        t_banks_fill(2)
+        for k in range(5):
+            dw_block(2, k, mx_banks[(k + 2) % 3])
+        rope_product(7, 3)
+        mean_terms(2)
+        rope_sum(7, 1, nc.vector)
+        feat_quantize(6)
+        tok_quantize(7)
+        norm_shift(0, 2)
+        dz_transpose(7, (3, 4), (nc.scalar.copy, nc.vector.tensor_copy))
+        dw_block(2, 5, 6)
+        dh_tile_passes(0, (1, 5), range(3))
         feat_quantize(7)
-        for k in range(2):
-            dh_passes(1, k, (6, 0)[k], range(3))
         norm_finish(0, 2)
-        for k in range(2):
-            dh_passes(1, k, None, [3])
-        tile_mean(0, 3, (7, 2))
-        for k in range(2, 4):
-            dh_passes(1, k, (3, 4)[k % 2], every_pass)
+        dh_tile_passes(0, None, [3])
+        t_banks_fill(3)
+        rest = [(2, k) for k in range(6, 8)] + [(3, k) for k in range(8)]
+        for fq, k in rest[0:2]:
+            dw_block(fq, k, (3, 4)[k % 2])
+        dh_tile_passes(1, (6, 0), every_pass)
+        tile_mean(0)
+        tile_gain(0)
+        mean_terms(3)
+        norm_shift(0, 3)
+        tile_finish(0)
+        for fq, k in rest[2:6]:
+            dw_block(fq, k, (3, 4)[k % 2])
+        dh_tile_passes(2, (1, 5), every_pass)
+        tile_mean(1)
+        tile_gain(1)
         norm_finish(0, 3)
-        for j in range(3):
-            dh_passes(1, 4 + j, (6, 0)[j % 2], every_pass)
-            t_transpose(1, j, 0, (1, 5, 3)[j])
-            norm_mean(1, j, 0)
-        dh_passes(1, 7, 0, every_pass)
-        rest = [(2, k) for k in range(4, 8)] + [(3, k) for k in range(8)]
-        dw_block(2, 4, 6)
-        for j in range(3):
-            t_transpose(1, j, 1, (4, 7, 2)[j])
-            norm_mean(1, j, 1)
-        for i in range(1, 4):
-            dw_block(rest[i][0], rest[i][1], (6, 0)[i % 2])
-        norm_finish(1, 0)
-        tile_mean(1, 3, (1, 4))
-        norm_finish(1, 1)
-        for i in range(4, 12):
-            dw_block(rest[i][0], rest[i][1], (6, 0)[i % 2])
-        norm_finish(1, 2)
-        norm_finish(1, 3)
+        tile_finish(1)
+        for fq, k in rest[6:8]:
+            dw_block(fq, k, (3, 4)[k % 2])
+        dh_tile_passes(3, (6, 0), every_pass)
+        for fq, k in rest[8:10]:
+            dw_block(fq, k, (3, 4)[k % 2])
+        tile_mean(2)
+        tile_gain(2)
+        last_tile_finish(2)
+        tile_mean(3)
+        tile_gain(3)
+        last_tile_finish(3)

@@ -66,17 +66,17 @@ def tile_attentionmodule_pa_v_kernel(tc, xs, norm_w, wq, wk, rstd, grad_0, grad_
 
         gain_rows = sbuf([P, P], BF16, "gain_rows")
         nc.vector.memset(gain_rows[:], 0.0)
-        nc.scalar.dma_start(out=gain_rows[0:8, :], in_=norm_w.rearrange("(k n) -> k n", n=P))
         r_sb = sbuf([P, 8], F32, "rstd")
         nc.sync.dma_start(out=r_sb[:].rearrange("p (g j) -> p g j", j=4), in_=rstd.rearrange("(g p j) o -> p g (j o)", p=P, j=4))
+        nc.sync.dma_start(out=gain_rows[0:8, :], in_=norm_w.rearrange("(k n) -> k n", n=P))
+        load_x(0)
         load_grad(0)
         load_weight(0)
-        load_x(0)
+        load_x(1)
         load_grad(1)
         load_weight(1)
         load_grad(2)
         load_weight(2)
-        load_x(1)
         load_grad(3)
         load_grad(4)
 
@@ -87,10 +87,23 @@ def tile_attentionmodule_pa_v_kernel(tc, xs, norm_w, wq, wk, rstd, grad_0, grad_
 
         one_zero = sbuf([P, 2], F32, "one_zero")
         nc.vector.memset(one_zero[:, 0:1], 1.0)
-        nc.vector.memset(one_zero[:, 1:2], 0.0)
+        zero = sbuf([P, 1], F32, "zero")
+        nc.vector.memset(zero[:], 0.0)
+        nc.scalar.activation(out=one_zero[:, 1:2], in_=zero[:], func=ACT.Sin)
+        is_cos = sbuf([P, 1], F32, "is_cos")
+        nc.vector.tensor_reduce(out=is_cos[:], in_=ident[:, 0:P:2], op=ALU.add, axis=AX.X)
+        ident_bf = sbuf([P, P], BF16, "ident_bf")
+        nc.vector.tensor_copy(out=ident_bf[:], in_=ident[:])
         quarter = sbuf([P, 1], F32, "quarter")
-        nc.vector.memset(quarter[0:64, :], 0.25)
-        nc.vector.memset(quarter[64:128, :], 0.0)
+        nc.vector.tensor_scalar(out=quarter[:], in0=is_cos[:], scalar1=0.25, scalar2=None, op0=ALU.mult)
+        phase = sbuf([P, 1], F32, "phase")
+        nc.vector.tensor_scalar(out=phase[:], in0=is_cos[:], scalar1=math.pi / 2, scalar2=None, op0=ALU.mult)
+        gain_ps = bank(2, BF16)
+        for k in range(8):
+            nc.tensor.matmul(out=gain_ps[:, P * k : P * (k + 1)], lhsT=ident_bf[:, k : k + 1].to_broadcast([P, P]), rhs=gain_rows[:], start=True, stop=True)
+        gain_t = bank(7, BF16)
+        nc.tensor.transpose(gain_t[:, 0:P], gain_rows[:], ident_bf[:])
+
         freq_rows = sbuf([P, PAIRS, 2], F32, "freq_rows")
         for col in range(PAIRS):
             u, q = divmod(col, 32)
@@ -101,13 +114,10 @@ def tile_attentionmodule_pa_v_kernel(tc, xs, norm_w, wq, wk, rstd, grad_0, grad_
                 nc.vector.tensor_scalar(out=freq_rows[:, col, :], in0=one_zero[:], scalar1=hi - lo, scalar2=lo, op0=ALU.mult, op1=ALU.add)
             else:
                 nc.scalar.activation(out=freq_rows[:, col, :], in_=one_zero[:], func=ACT.Copy, scale=hi - lo, bias=lo)
-        nc.scalar.activation(out=pos[:, PASS:S], in_=pos[:, 0:PASS], func=ACT.Copy, bias=float(PASS))
+        gain_wide = sbuf([P, D], BF16, "gain_wide")
+        nc.scalar.copy(out=gain_wide[:], in_=gain_ps[:])
         pick = sbuf([P, PAIRS], F32, "pick")
-        nc.vector.tensor_tensor(out=pick[:], in0=ident[:, 0:PAIRS], in1=ident[:, PAIRS:P], op=ALU.add)
-        ident_bf = sbuf([P, P], BF16, "ident_bf")
-        nc.vector.tensor_copy(out=ident_bf[:], in_=ident[:])
-        phase = sbuf([P, 1], F32, "phase")
-        nc.vector.tensor_scalar(out=phase[:], in0=quarter[:], scalar1=2 * math.pi, scalar2=None, op0=ALU.mult)
+        nc.vector.tensor_tensor(out=pick[:], in0=ident[:, 0:P:2], in1=ident[:, 1:P:2], op=ALU.add)
         picked = sbuf([P, PAIRS, 2], F32, "picked")
         nc.vector.tensor_tensor(out=picked[:], in0=freq_rows[:], in1=pick[:].unsqueeze(2).broadcast_to([P, PAIRS, 2]), op=ALU.mult)
         freq = sbuf([P, 1], F32, "freq")
@@ -139,28 +149,35 @@ def tile_attentionmodule_pa_v_kernel(tc, xs, norm_w, wq, wk, rstd, grad_0, grad_
 
         neg_r2 = sbuf([P, 8], F32, "neg_r2")
         neg_r3 = sbuf([P, 8], F32, "neg_r3")
-        whole_turns(0)
-        whole_turns(1)
-        frac_high(0)
-        nc.vector.scalar_tensor_tensor(out=neg_r2[:], in0=r_sb[:], scalar=-1.0 / D, in1=r_sb[:], op0=ALU.mult, op1=ALU.mult)
-        frac_low(0)
-        table_to_psum(0, 0)
-        frac_high(1)
-        nc.vector.tensor_tensor(out=neg_r3[:], in0=neg_r2[:], in1=r_sb[:], op=ALU.mult)
         gain_col = sbuf([P, 8], F32, "gain_col")
 
-        h_raw, h_mix, h_q = {}, {}, {}
+        h_raw, h_mix, h_q, x_hat = {}, {}, {}, {}
 
         def h_slot(g, j):
+            cols = (halves[1], slice(0, D))[g]
+            width = cols.stop - cols.start
             if j == 0:
-                h_raw[g] = sbuf([P, 4 * D], (BF16, F32)[g], "h_raw%d" % g)
-            cols = slice(D * j, D * (j + 1))
-            nc.vector.scalar_tensor_tensor(out=h_raw[g][:, cols], in0=x_sb[g][:, cols], scalar=r_sb[:, 4 * g + j : 4 * g + j + 1], in1=gain_ps[:], op0=ALU.mult, op1=ALU.mult)
+                h_raw[g] = sbuf([P, 4 * width], (BF16, F32)[g], "h_raw%d" % g)
+            nc.vector.scalar_tensor_tensor(out=h_raw[g][:, width * j : width * (j + 1)], in0=x_sb[g][:, D * j + cols.start : D * j + cols.stop],
+                                           scalar=r_sb[:, 4 * g + j : 4 * g + j + 1], in1=gain_ps[:, cols], op0=ALU.mult, op1=ALU.mult)
 
         def h_interleave(g, half):
             h_mix[g, half] = sbuf([P, 4 * PASS], BF16, "h_mix", 3)
-            src = h_raw[g][:].rearrange("p (j a c i) -> p a c j i", j=4, a=2, i=4)[:, half]
+            src = h_raw[g][:].rearrange("p (j a c i) -> p a c j i", j=4, c=P, i=4)[:, half if g else 0]
             nc.scalar.copy(out=h_mix[g, half][:].rearrange("p (c i j) -> p c j i", i=4, j=4), in_=src)
+
+        def x_normalise(part):
+            x_hat[part] = sbuf([P, 4 * 256], F32, "prod", 5)
+            for j in range(4):
+                nc.scalar.activation(out=x_hat[part][:, 256 * j : 256 * (j + 1)], in_=x_sb[0][:, D * j + 256 * part : D * j + 256 * (part + 1)],
+                                     func=ACT.Copy, scale=r_sb[:, j : j + 1])
+
+        def h_from_x_hat(part):
+            if part == 0:
+                h_mix[0, 0] = sbuf([P, 4 * PASS], BF16, "h_mix", 3)
+            out = h_mix[0, 0][:, D * part : D * (part + 1)].rearrange("p (c i j) -> p c j i", i=4, j=4)
+            gain = gain_wide[:, 256 * part : 256 * (part + 1)].rearrange("p (c i) -> p c i", i=4).unsqueeze(2).broadcast_to([P, 64, 4, 4])
+            nc.gpsimd.tensor_tensor(out=out, in0=x_hat[part][:].rearrange("p (j c i) -> p c j i", j=4, i=4), in1=gain, op=ALU.mult)
 
         def quantize(src, fmt, tag, bufs):
             codes = sbuf([P, PASS], U32, tag + "_codes", bufs)
@@ -194,20 +211,23 @@ def tile_attentionmodule_pa_v_kernel(tc, xs, norm_w, wq, wk, rstd, grad_0, grad_
         def rope_product(n, t, heads=slice(0, 4)):
             if heads.start == 0:
                 prod[n, t] = sbuf([P, 2 * PASS], F32, "prod", 5)
-            shape = [P, 4, 2, heads.stop - heads.start, 32]
+            shape = [P, 4, heads.stop - heads.start, 32, 2]
             src = g_sb[n][:].rearrange("p (j h q t) -> p t j h q", j=4, h=4, t=4)[:, t, :, heads]
-            factor = tab[n // 4][:].rearrange("p (j l u q) -> p u j l q", j=4, l=2, u=2)[:, t // 2]
-            out = prod[n, t][:].rearrange("p (j l h q) -> p j l h q", j=4, l=2, h=4)[:, :, :, heads]
-            nc.vector.tensor_tensor(out=out, in0=src.unsqueeze(2).broadcast_to(shape), in1=factor.unsqueeze(3).broadcast_to(shape), op=ALU.mult)
+            factor = tab[n // 4][:].rearrange("p (j u q l) -> p u j q l", j=4, u=2, l=2)[:, t // 2]
+            out = prod[n, t][:].rearrange("p (j h q l) -> p j h q l", j=4, h=4, l=2)[:, :, heads]
+            nc.vector.tensor_tensor(out=out, in0=src.unsqueeze(4).broadcast_to(shape), in1=factor.unsqueeze(2).broadcast_to(shape), op=ALU.mult)
 
-        def rope_sum(n, u, engine):
-            if u == 0:
+        def rope_add(n, t, engine):
+            if t == 0:
                 dz_tok[n] = sbuf([P, 4 * PASS], BF16, "dz_tok", 3)
-            even = prod[n, 2 * u][:].rearrange("p (j l c i) -> p l c j i", j=4, l=2, i=4)
-            odd = prod[n, 2 * u + 1][:].rearrange("p (j l c i) -> p l c j i", j=4, l=2, i=4)
-            out = dz_tok[n][:].rearrange("p (t c i j) -> p t c j i", t=4, i=4, j=4)
-            engine.tensor_tensor(out=out[:, 2 * u], in0=even[:, 0], in1=odd[:, 1], op=ALU.add)
-            engine.tensor_tensor(out=out[:, 2 * u + 1], in0=odd[:, 0], in1=even[:, 1], op=ALU.subtract)
+            by_cos = prod[n, t][:].rearrange("p (j c i l) -> p l c j i", j=4, i=4, l=2)[:, 0]
+            by_sin = prod[n, t ^ 1][:].rearrange("p (j c i l) -> p l c j i", j=4, i=4, l=2)[:, 1]
+            out = dz_tok[n][:].rearrange("p (t c i j) -> p t c j i", t=4, i=4, j=4)[:, t]
+            engine.tensor_tensor(out=out, in0=by_cos, in1=by_sin, op=(ALU.add, ALU.subtract)[t % 2])
+
+        def rope_sum(n, u, engines):
+            for e in range(len(engines)):
+                rope_add(n, 2 * u + e, engines[e])
 
         def dz_transpose(n, banks, copies=(nc.scalar.copy, nc.scalar.copy)):
             dz_feat[n] = sbuf([P, 4 * PASS], BF16, "dz_feat", 2)
@@ -344,18 +364,20 @@ def tile_attentionmodule_pa_v_kernel(tc, xs, norm_w, wq, wk, rstd, grad_0, grad_
                 nc.vector.scalar_tensor_tensor(out=part, in0=t_tok[g, j, half][:], scalar=r_sb[:, slot], in1=part, op0=ALU.mult, op1=ALU.add)
             nc.sync.dma_start(out=dx_hbm[g, j], in_=dx[g, j][:])
 
+        on_gpsimd = (nc.gpsimd, nc.gpsimd)
+
         def first_products(n):
             rope_product(n, 0)
             rope_product(n, 1)
-            rope_sum(n, 0, nc.gpsimd)
+            rope_sum(n, 0, on_gpsimd)
 
         def second_products(n):
             rope_product(n, 2)
             rope_product(n, 3, slice(0, 3))
 
-        def close_chunk(n, engine):
+        def close_chunk(n):
             rope_product(n, 3, slice(3, 4))
-            rope_sum(n, 1, engine)
+            rope_sum(n, 1, on_gpsimd)
             if n + 5 < 8:
                 load_grad(n + 5)
 
@@ -370,62 +392,69 @@ def tile_attentionmodule_pa_v_kernel(tc, xs, norm_w, wq, wk, rstd, grad_0, grad_
         every_pass = range(4)
         mx_banks = (5, 6, 0)
 
-        frac_low(1)
-        gain_ps = bank(2, BF16)
-        for k in range(8):
-            nc.tensor.matmul(out=gain_ps[:, P * k : P * (k + 1)], lhsT=ident_bf[:, k : k + 1].to_broadcast([P, P]), rhs=gain_rows[:], start=True, stop=True)
-        gain_t = bank(7, BF16)
-        nc.tensor.transpose(gain_t[:, 0:P], gain_rows[:], ident_bf[:])
-
+        whole_turns(0)
+        nc.vector.scalar_tensor_tensor(out=neg_r2[:], in0=r_sb[:], scalar=-1.0 / D, in1=r_sb[:], op0=ALU.mult, op1=ALU.mult)
+        frac_high(0)
+        nc.vector.tensor_tensor(out=neg_r3[:], in0=neg_r2[:], in1=r_sb[:], op=ALU.mult)
+        x_normalise(0)
+        frac_low(0)
+        table_to_psum(0, 0)
+        x_normalise(1)
+        for part in range(2):
+            h_from_x_hat(part)
+        for j in range(4):
+            h_slot(0, j)
+        nc.scalar.activation(out=pos[:, PASS:S], in_=pos[:, 0:PASS], func=ACT.Copy, bias=float(PASS))
         w_transpose(0, 0, (3, 4))
         w_transpose(0, 1, (5, 6))
         nc.scalar.copy(out=gain_col[:], in_=gain_t[:, 0:8])
         load_weight(3)
-        h_first = ((0, 0), (0, 2), (1, 0), (1, 1))
         for n in range(4):
-            if n == 2:
-                h_interleave(0, 0)
+            if n == 1:
+                h_interleave(0, 1)
             first_products(n)
             second_products(n)
-            h_slot(*h_first[n])
+            h_slot(1, n)
             if n > 0:
                 dz_transpose(n - 1, (3, 4))
                 tok_quantize(n - 1)
+            if n == 0:
+                whole_turns(1)
             w_quantize(n, 0)
+            if n == 0:
+                frac_high(1)
             w_quantize(n, 1)
+            if n == 0:
+                frac_low(1)
             if n < 3:
                 w_transpose(n + 1, 0, (5, 1))
                 w_transpose(n + 1, 1, (3, 4))
-            if n == 2:
-                gain_wide = sbuf([P, D], BF16, "gain_wide")
-                nc.scalar.copy(out=gain_wide[:], in_=gain_ps[:])
+            if n in (1, 2):
+                h_quantize(0, n - 1)
             if n == 3:
                 table_to_psum(1, 1)
-                h_interleave(0, 1)
                 dh_passes(0, 2, 5, range(2))
-            close_chunk(n, nc.gpsimd)
+            close_chunk(n)
             if n > 0:
                 feat_quantize(n - 1)
                 for k in range(2 if n < 3 else 3):
                     dh_passes(0, k, (6, 7, 5)[k], [n - 1])
-            if n < 2:
-                h_slot(0, 2 * n + 1)
-        first_products(4)
-        h_slot(1, 2)
-        h_slot(1, 3)
-        dh_passes(0, 3, 0, range(3))
-        dz_transpose(3, (3, 4))
-        dh_passes(0, 4, 2, range(3))
         h_interleave(1, 0)
+        rope_product(4, 0)
+        rope_product(4, 1)
+        rope_add(4, 0, nc.gpsimd)
+        for k in range(3, 5):
+            dh_passes(0, k, (0, 2)[k - 3], range(3))
+        dz_transpose(3, (3, 4))
+        h_interleave(1, 1)
         second_products(4)
+        rope_add(4, 1, nc.vector)
         tok_quantize(3)
-        h_quantize(0, 0)
-        h_quantize(0, 1)
-        close_chunk(4, nc.gpsimd)
+        h_quantize(1, 0)
+        close_chunk(4)
         feat_quantize(3)
         for k in range(3):
             dh_passes(0, k, None, [3])
-        h_interleave(1, 1)
         first_products(5)
         for k in range(3, 5):
             dh_passes(0, k, None, [3])
@@ -436,25 +465,25 @@ def tile_attentionmodule_pa_v_kernel(tc, xs, norm_w, wq, wk, rstd, grad_0, grad_
         t_banks_fill(0)
         second_products(5)
         tok_quantize(4)
-        h_quantize(1, 0)
         h_quantize(1, 1)
-        close_chunk(5, nc.gpsimd)
+        close_chunk(5)
         for k in range(4):
             dw_block(0, k, mx_banks[(k + 1) % 3])
         rope_product(6, 0)
         mean_terms(0)
         rope_product(6, 1)
         norm_shift(0, 0)
-        rope_sum(6, 0, nc.gpsimd)
+        rope_add(6, 0, nc.gpsimd)
         dz_transpose(5, (3, 4))
         for k in range(4, 8):
             dw_block(0, k, mx_banks[(k + 1) % 3])
         second_products(6)
         norm_finish(0, 0)
         t_banks_fill(1)
+        rope_add(6, 1, nc.vector)
         feat_quantize(4)
         tok_quantize(5)
-        close_chunk(6, nc.gpsimd)
+        close_chunk(6)
         feat_quantize(5)
         for k in range(4):
             dw_block(1, k, mx_banks[k % 3])
@@ -468,14 +497,14 @@ def tile_attentionmodule_pa_v_kernel(tc, xs, norm_w, wq, wk, rstd, grad_0, grad_
         rope_product(7, 2)
         tok_quantize(6)
         rope_product(7, 1, slice(3, 4))
-        rope_sum(7, 0, nc.gpsimd)
+        rope_sum(7, 0, on_gpsimd)
         norm_finish(0, 1)
         t_banks_fill(2)
         for k in range(5):
             dw_block(2, k, mx_banks[(k + 2) % 3])
         rope_product(7, 3)
         mean_terms(2)
-        rope_sum(7, 1, nc.vector)
+        rope_sum(7, 1, (nc.vector, nc.vector))
         feat_quantize(6)
         tok_quantize(7)
         norm_shift(0, 2)

@@ -145,7 +145,7 @@ def tile_attentionmodule_pa_v_kernel(tc, xs, norm_w, wq, wk, rstd, grad_0, grad_
         def table_to_psum(g, b):
             tab[g] = bank(b)
             for j in range(4):
-                nc.tensor.transpose(tab[g][:, P * j : P * (j + 1)], table[:, PASS * g + P * j : PASS * g + P * (j + 1)], ident[:])
+                nc.tensor.transpose(tab[g][:].rearrange("p (c j l) -> p j c l", j=4, l=2)[:, j], table[:, PASS * g + P * j : PASS * g + P * (j + 1)], ident[:])
 
         neg_r2 = sbuf([P, 8], F32, "neg_r2")
         neg_r3 = sbuf([P, 8], F32, "neg_r3")
@@ -211,19 +211,18 @@ def tile_attentionmodule_pa_v_kernel(tc, xs, norm_w, wq, wk, rstd, grad_0, grad_
         def rope_product(n, t, heads=slice(0, 4)):
             if heads.start == 0:
                 prod[n, t] = sbuf([P, 2 * PASS], F32, "prod", 5)
-            shape = [P, 4, heads.stop - heads.start, 32, 2]
-            src = g_sb[n][:].rearrange("p (j h q t) -> p t j h q", j=4, h=4, t=4)[:, t, :, heads]
-            factor = tab[n // 4][:].rearrange("p (j u q l) -> p u j q l", j=4, u=2, l=2)[:, t // 2]
-            out = prod[n, t][:].rearrange("p (j h q l) -> p j h q l", j=4, h=4, l=2)[:, :, heads]
-            nc.vector.tensor_tensor(out=out, in0=src.unsqueeze(4).broadcast_to(shape), in1=factor.unsqueeze(2).broadcast_to(shape), op=ALU.mult)
+            shape = [P, heads.stop - heads.start, 32, 4, 2]
+            src = g_sb[n][:].rearrange("p (j h q t) -> p t h q j", j=4, h=4, t=4)[:, t, heads]
+            factor = tab[n // 4][:].rearrange("p (u q j l) -> p u q j l", u=2, j=4, l=2)[:, t // 2]
+            out = prod[n, t][:].rearrange("p (h q j l) -> p h q j l", h=4, j=4, l=2)[:, heads]
+            nc.vector.tensor_tensor(out=out, in0=src.unsqueeze(4).broadcast_to(shape), in1=factor.unsqueeze(1).broadcast_to(shape), op=ALU.mult)
 
         def rope_add(n, t, engine):
             if t == 0:
                 dz_tok[n] = sbuf([P, 4 * PASS], BF16, "dz_tok", 3)
-            by_cos = prod[n, t][:].rearrange("p (j c i l) -> p l c j i", j=4, i=4, l=2)[:, 0]
-            by_sin = prod[n, t ^ 1][:].rearrange("p (j c i l) -> p l c j i", j=4, i=4, l=2)[:, 1]
-            out = dz_tok[n][:].rearrange("p (t c i j) -> p t c j i", t=4, i=4, j=4)[:, t]
-            engine.tensor_tensor(out=out, in0=by_cos, in1=by_sin, op=(ALU.add, ALU.subtract)[t % 2])
+            by_cos = prod[n, t][:, 0 : 2 * PASS : 2]
+            by_sin = prod[n, t ^ 1][:, 1 : 2 * PASS : 2]
+            engine.tensor_tensor(out=dz_tok[n][:, PASS * t : PASS * (t + 1)], in0=by_cos, in1=by_sin, op=(ALU.add, ALU.subtract)[t % 2])
 
         def rope_sum(n, u, engines):
             for e in range(len(engines)):

import math
from contextlib import ExitStack

import concourse.mybir as mybir
from concourse.masks import make_identity

S, D, NH, HD = 1024, 1024, 8, 128
F = NH * HD
ROPE_BASE = 10000.0
FLOPS = 2 * 2 * S * D * 2 * F

F32 = mybir.dt.float32
BF16 = mybir.dt.bfloat16
I32 = mybir.dt.int32
U32 = mybir.dt.uint32
U8 = mybir.dt.uint8
E4M3 = mybir.dt.float8_e4m3fn_x4
E5M2 = mybir.dt.float8_e5m2_x4
ALU = mybir.AluOpType
ACT = mybir.ActivationFunctionType
AX = mybir.AxisListType

P = 128
PASS = 512
PAIRS = HD // 2
VECTOR_COLUMNS = 30
ON_VECTOR = (3, 4)


def tile_attentionmodule_pa_v_kernel(tc, xs, norm_w, wq, wk, rstd, grad_0, grad_1, out_0, out_1, out_2):
    nc = tc.nc
    with ExitStack() as ctx:
        sb = ctx.enter_context(tc.tile_pool(name="sb", bufs=1))
        ps = ctx.enter_context(tc.psum_pool(name="ps", bufs=1))
        ctx.enter_context(tc.manual_schedule())

        def sbuf(shape, dtype, tag, bufs=1):
            return sb.tile(shape, dtype, name=tag, tag=tag, bufs=bufs, align_bytes=64)

        def bank(b, dtype=F32):
            width = PASS if dtype == F32 else 2 * PASS
            return ps.tile([P, width], dtype, name="bank%d" % b, tag="bank%d" % b)

        grads = [t.rearrange("(g p j) n h -> g p j (n h)", p=P, j=4) for t in (grad_0, grad_1)]
        weights = [t.rearrange("(k p) n h -> p k (n h)", p=P) for t in (wq, wk)]
        dws = [t.rearrange("(k p) n h -> p k (n h)", p=P) for t in (out_1, out_2)]
        x_hbm = xs.rearrange("(g p j) d -> g p (j d)", p=P, j=4)
        dx_hbm = out_0.rearrange("(g p j) d -> g j p d", p=P, j=4)

        g_sb, w_sb, x_sb = {}, {}, {}

        def load_grad(n):
            g, fq = divmod(n, 4)
            g_sb[n] = sbuf([P, 4 * PASS], BF16, "grad", 5)
            cols = slice(PASS * (fq % 2), PASS * (fq % 2 + 1))
            nc.sync.dma_start(out=g_sb[n][:].rearrange("p (j f) -> p j f", j=4), in_=grads[fq // 2][g][:, :, cols])

        def load_weight(fq):
            w_sb[fq] = sbuf([P, 8 * PASS], BF16, "big", 3)
            cols = slice(PASS * (fq % 2), PASS * (fq % 2 + 1))
            nc.sync.dma_start(out=w_sb[fq][:].rearrange("p (k f) -> p k f", k=8), in_=weights[fq // 2][:, :, cols])

        def load_x(g):
            x_sb[g] = sbuf([P, 4 * D], BF16, "x", 2)
            nc.sync.dma_start(out=x_sb[g][:], in_=x_hbm[g])

        gain_rows = sbuf([P, P], BF16, "gain_rows")
        nc.vector.memset(gain_rows[:], 0.0)
        r_sb = sbuf([P, 8], F32, "rstd")
        nc.sync.dma_start(out=r_sb[:].rearrange("p (g j) -> p g j", j=4), in_=rstd.rearrange("(g p j) o -> p g (j o)", p=P, j=4))
        nc.sync.dma_start(out=gain_rows[0:8, :], in_=norm_w.rearrange("(k n) -> k n", n=P))
        load_x(0)
        load_grad(0)
        load_weight(0)
        load_x(1)
        load_grad(1)
        load_weight(1)
        load_grad(2)
        load_weight(2)
        load_grad(3)
        load_grad(4)

        ident = sbuf([P, P], F32, "ident")
        make_identity(nc, ident[:])
        pos = sbuf([P, S], F32, "stage", 6)
        nc.gpsimd.iota(pos[:, 0:PASS], pattern=[[1, 4], [4, P]], base=0, channel_multiplier=0, allow_small_or_imprecise_dtypes=True)

        one_zero = sbuf([P, 2], F32, "one_zero")
        nc.vector.memset(one_zero[:, 0:1], 1.0)
        zero = sbuf([P, 1], F32, "zero")
        nc.vector.memset(zero[:], 0.0)
        nc.scalar.activation(out=one_zero[:, 1:2], in_=zero[:], func=ACT.Sin)
        is_cos = sbuf([P, 1], F32, "is_cos")
        nc.vector.tensor_reduce(out=is_cos[:], in_=ident[:, 0:P:2], op=ALU.add, axis=AX.X)
        ident_bf = sbuf([P, P], BF16, "ident_bf")
        nc.vector.tensor_copy(out=ident_bf[:], in_=ident[:])
        quarter = sbuf([P, 1], F32, "quarter")
        nc.vector.tensor_scalar(out=quarter[:], in0=is_cos[:], scalar1=0.25, scalar2=None, op0=ALU.mult)
        phase = sbuf([P, 1], F32, "phase")
        nc.vector.tensor_scalar(out=phase[:], in0=is_cos[:], scalar1=math.pi / 2, scalar2=None, op0=ALU.mult)
        gain_ps = bank(2, BF16)
        for k in range(8):
            nc.tensor.matmul(out=gain_ps[:, P * k : P * (k + 1)], lhsT=ident_bf[:, k : k + 1].to_broadcast([P, P]), rhs=gain_rows[:], start=True, stop=True)
        gain_t = bank(7, BF16)
        nc.tensor.transpose(gain_t[:, 0:P], gain_rows[:], ident_bf[:])

        freq_rows = sbuf([P, PAIRS, 2], F32, "freq_rows")
        for col in range(PAIRS):
            u, q = divmod(col, 32)
            turns = 1.0 / ROPE_BASE ** (2 * (2 * q + u) / HD) / (2 * math.pi)
            hi = math.floor(turns * 65536) / 65536
            lo = turns - hi
            if col < VECTOR_COLUMNS:
                nc.vector.tensor_scalar(out=freq_rows[:, col, :], in0=one_zero[:], scalar1=hi - lo, scalar2=lo, op0=ALU.mult, op1=ALU.add)
            else:
                nc.scalar.activation(out=freq_rows[:, col, :], in_=one_zero[:], func=ACT.Copy, scale=hi - lo, bias=lo)
        gain_wide = sbuf([P, D], BF16, "gain_wide")
        nc.scalar.copy(out=gain_wide[:], in_=gain_ps[:])
        pick = sbuf([P, PAIRS], F32, "pick")
        nc.vector.tensor_tensor(out=pick[:], in0=ident[:, 0:P:2], in1=ident[:, 1:P:2], op=ALU.add)
        picked = sbuf([P, PAIRS, 2], F32, "picked")
        nc.vector.tensor_tensor(out=picked[:], in0=freq_rows[:], in1=pick[:].unsqueeze(2).broadcast_to([P, PAIRS, 2]), op=ALU.mult)
        freq = sbuf([P, 1], F32, "freq")
        nc.vector.tensor_reduce(out=freq[:], in_=picked[:].rearrange("p c l -> p (c l)"), op=ALU.add, axis=AX.X)
        freq_parts = sbuf([P, 2], F32, "freq_parts")
        nc.vector.tensor_reduce(out=freq_parts[:], in_=picked[:].rearrange("p c l -> p l c"), op=ALU.add, axis=AX.X)

        whole = sbuf([P, S], I32, "stage", 6)
        frac = sbuf([P, S], F32, "stage", 6)
        table = sbuf([P, S], F32, "stage", 6)
        halves = [slice(0, PASS), slice(PASS, S)]

        def whole_turns(g):
            nc.vector.tensor_scalar(out=whole[:, halves[g]], in0=pos[:, halves[g]], scalar1=freq[:], scalar2=quarter[:], op0=ALU.mult, op1=ALU.add)

        def frac_high(g):
            nc.vector.scalar_tensor_tensor(out=frac[:, halves[g]], in0=pos[:, halves[g]], scalar=freq_parts[:, 0:1], in1=whole[:, halves[g]], op0=ALU.mult, op1=ALU.subtract)

        def frac_low(g):
            nc.vector.scalar_tensor_tensor(out=frac[:, halves[g]], in0=pos[:, halves[g]], scalar=freq_parts[:, 1:2], in1=frac[:, halves[g]], op0=ALU.mult, op1=ALU.add)
            nc.scalar.activation(out=table[:, halves[g]], in_=frac[:, halves[g]], func=ACT.Sin, scale=2 * math.pi, bias=phase[:])

        tab = {}

        def table_to_psum(g, b):
            tab[g] = bank(b)
            for j in range(4):
                nc.tensor.transpose(tab[g][:].rearrange("p (c j l) -> p j c l", j=4, l=2)[:, j], table[:, PASS * g + P * j : PASS * g + P * (j + 1)], ident[:])

        neg_r2 = sbuf([P, 8], F32, "neg_r2")
        neg_r3 = sbuf([P, 8], F32, "neg_r3")
        gain_col = sbuf([P, 8], F32, "gain_col")

        h_raw, h_mix, h_q, x_hat = {}, {}, {}, {}

        def h_slot(g, j):
            cols = (halves[1], slice(0, D))[g]
            width = cols.stop - cols.start
            if j == 0:
                h_raw[g] = sbuf([P, 4 * width], (BF16, F32)[g], "h_raw%d" % g)
            nc.vector.scalar_tensor_tensor(out=h_raw[g][:, width * j : width * (j + 1)], in0=x_sb[g][:, D * j + cols.start : D * j + cols.stop],
                                           scalar=r_sb[:, 4 * g + j : 4 * g + j + 1], in1=gain_ps[:, cols], op0=ALU.mult, op1=ALU.mult)

        def h_interleave(g, half):
            h_mix[g, half] = sbuf([P, 4 * PASS], BF16, "h_mix", 3)
            src = h_raw[g][:].rearrange("p (j a c i) -> p a c j i", j=4, c=P, i=4)[:, half if g else 0]
            nc.scalar.copy(out=h_mix[g, half][:].rearrange("p (c i j) -> p c j i", i=4, j=4), in_=src)

        def x_normalise(part):
            x_hat[part] = sbuf([P, 4 * 256], F32, "prod", 5)
            for j in range(4):
                nc.scalar.activation(out=x_hat[part][:, 256 * j : 256 * (j + 1)], in_=x_sb[0][:, D * j + 256 * part : D * j + 256 * (part + 1)],
                                     func=ACT.Copy, scale=r_sb[:, j : j + 1])

        def h_from_x_hat(part):
            if part == 0:
                h_mix[0, 0] = sbuf([P, 4 * PASS], BF16, "h_mix", 3)
            out = h_mix[0, 0][:, D * part : D * (part + 1)].rearrange("p (c i j) -> p c j i", i=4, j=4)
            gain = gain_wide[:, 256 * part : 256 * (part + 1)].rearrange("p (c i) -> p c i", i=4).unsqueeze(2).broadcast_to([P, 64, 4, 4])
            nc.gpsimd.tensor_tensor(out=out, in0=x_hat[part][:].rearrange("p (j c i) -> p c j i", j=4, i=4), in1=gain, op=ALU.mult)

        def quantize(src, fmt, tag, bufs):
            codes = sbuf([P, PASS], U32, tag + "_codes", bufs)
            scales = sbuf([P, PASS], U8, tag + "_scales", bufs)
            nc.vector.quantize_mx(out=codes[:].bitcast(fmt), scales=scales[:], in_=src[:])
            return codes, scales

        def h_quantize(g, half):
            h_q[g, half] = quantize(h_mix[g, half], E4M3, "h", 4)

        w_mix, w_q = {}, {}

        def w_transpose(fq, half, banks):
            w_mix[fq, half] = sbuf([P, 4 * PASS], BF16, "w_mix", 2)
            words = w_sb[fq][:].bitcast(F32)
            mixed = w_mix[fq, half][:].bitcast(F32).rearrange("p (b k d u) -> p b k d u", b=2, k=2, u=2)
            for b in range(2):
                turned = bank(banks[b])
                for kk in range(2):
                    k = 4 * half + 2 * b + kk
                    for u in range(2):
                        at = P * (2 * kk + u)
                        nc.tensor.transpose(turned[:, at : at + P], words[:, 256 * k + u : 256 * (k + 1) : 2], ident[:])
                nc.scalar.copy(out=mixed[:, b], in_=turned[:].rearrange("p (k u d) -> p k d u", k=2, u=2))

        def w_quantize(fq, half):
            w_q[fq, half] = quantize(w_mix[fq, half], E4M3, "w", 8)

        prod, dz_tok, dz_feat, dz_tok_q, dz_feat_q = {}, {}, {}, {}, {}

        def rope_product(n, t, heads=slice(0, 4)):
            if heads.start == 0:
                prod[n, t] = sbuf([P, 2 * PASS], F32, "prod", 5)
            shape = [P, heads.stop - heads.start, 32, 4, 2]
            src = g_sb[n][:].rearrange("p (j h q t) -> p t h q j", j=4, h=4, t=4)[:, t, heads]
            factor = tab[n // 4][:].rearrange("p (u q j l) -> p u q j l", u=2, j=4, l=2)[:, t // 2]
            out = prod[n, t][:].rearrange("p (h q j l) -> p h q j l", h=4, j=4, l=2)[:, heads]
            nc.vector.tensor_tensor(out=out, in0=src.unsqueeze(4).broadcast_to(shape), in1=factor.unsqueeze(1).broadcast_to(shape), op=ALU.mult)

        def rope_add(n, t, engine):
            if t == 0:
                dz_tok[n] = sbuf([P, 4 * PASS], BF16, "dz_tok", 3)
            by_cos = prod[n, t][:, 0 : 2 * PASS : 2]
            by_sin = prod[n, t ^ 1][:, 1 : 2 * PASS : 2]
            engine.tensor_tensor(out=dz_tok[n][:, PASS * t : PASS * (t + 1)], in0=by_cos, in1=by_sin, op=(ALU.add, ALU.subtract)[t % 2])

        def rope_sum(n, u, engines):
            for e in range(len(engines)):
                rope_add(n, 2 * u + e, engines[e])

        def dz_transpose(n, banks, copies=(nc.scalar.copy, nc.scalar.copy)):
            dz_feat[n] = sbuf([P, 4 * PASS], BF16, "dz_feat", 2)
            words = dz_tok[n][:].bitcast(F32)
            for jp in range(2):
                turned = bank(banks[jp])
                for t in range(4):
                    nc.tensor.transpose(turned[:, P * t : P * (t + 1)], words[:, 256 * t + jp : 256 * (t + 1) : 2], ident[:])
                out = dz_feat[n][:].rearrange("r (a e p t) -> r a e p t", a=2, e=2, t=4)[:, jp]
                copies[jp](out=out, in_=turned[:].bitcast(BF16).rearrange("r (t p e) -> r e p t", t=4, e=2))

        def tok_quantize(n):
            dz_tok_q[n] = quantize(dz_tok[n], E5M2, "dz_tok", 6)

        def feat_quantize(n):
            dz_feat_q[n] = quantize(dz_feat[n], E5M2, "dz_feat", 6)

        t_feat = {}

        dh_acc = {}

        def dh_passes(g, k, b, passes):
            if passes[0] == 0:
                dh_acc[g, k] = bank(b)
            acc = dh_acc[g, k]
            cols = slice(P * (k % 4), P * (k % 4 + 1))
            for fq in passes:
                w_codes, w_scales = w_q[fq, k // 4]
                z_codes, z_scales = dz_feat_q[4 * g + fq]
                nc.tensor.matmul_mx(out=acc[:], lhsT=w_codes[:, cols].bitcast(E4M3), lhsT_scale=w_scales[:, cols],
                                    rhs=z_codes[:].bitcast(E5M2), rhs_scale=z_scales[:], start=(fq == 0), stop=(fq == 3))
            if passes[-1] < 3:
                return
            if k % 4 == 0:
                t_feat[g, k // 4] = sbuf([P, 4 * PASS], F32, "big", 3)
            out = t_feat[g, k // 4][:, PASS * (k % 4) : PASS * (k % 4 + 1)]
            if k in ON_VECTOR:
                nc.vector.tensor_scalar(out=out, in0=acc[:], scalar1=gain_col[:, k : k + 1], scalar2=None, op0=ALU.mult)
            else:
                nc.scalar.activation(out=out, in_=acc[:], func=ACT.Copy, scale=gain_col[:, k : k + 1])

        dw_stage = {}

        def dw_block(fq, k, b):
            if k % 2 == 0:
                dw_stage[fq, k // 2] = sbuf([P, 2 * PASS], F32, "stage", 6)
            stage = dw_stage[fq, k // 2]
            acc = bank(b)
            cols = slice(P * (k % 4), P * (k % 4 + 1))
            for g in range(2):
                h_codes, h_scales = h_q[g, k // 4]
                z_codes, z_scales = dz_tok_q[4 * g + fq]
                nc.tensor.matmul_mx(out=acc[:], lhsT=h_codes[:, cols].bitcast(E4M3), lhsT_scale=h_scales[:, cols],
                                    rhs=z_codes[:].bitcast(E5M2), rhs_scale=z_scales[:], start=(g == 0), stop=(g == 1))
            out = stage[:, PASS * (k % 2) : PASS * (k % 2 + 1)].rearrange("p (r t) -> p r t", t=4)
            nc.scalar.copy(out=out, in_=acc[:].rearrange("p (t r) -> p r t", t=4))
            if k % 2 == 1:
                feats = slice(PASS * (fq % 2), PASS * (fq % 2 + 1))
                nc.sync.dma_start(out=dws[fq // 2][:, k - 1 : k + 1, feats], in_=stage[:].rearrange("p (k f) -> p k f", k=2))

        t_tok, dx = {}, {}

        def t_transpose(g, j, half, b):
            t_tok[g, j, half] = bank(b)
            for kk in range(4):
                at = PASS * kk + P * j
                nc.tensor.transpose(t_tok[g, j, half][:, P * kk : P * (kk + 1)], t_feat[g, half][:, at : at + P], ident[:])

        sums = {}

        def norm_mean(g, j, half):
            slot = slice(4 * g + j, 4 * g + j + 1)
            if half == 0:
                dx[g, j] = sbuf([P, D], F32, "grad", 5)
                sums[g, j] = sbuf([P, 2], F32, "sums", 4)
            nc.vector.scalar_tensor_tensor(out=dx[g, j][:, halves[half]], in0=t_tok[g, j, half][:], scalar=neg_r3[:, slot],
                                           in1=x_sb[g][:, D * j + PASS * half : D * j + PASS * (half + 1)],
                                           op0=ALU.mult, op1=ALU.mult, accum_out=sums[g, j][:, half : half + 1])

        def norm_shift(g, j):
            coef = sbuf([P, 1], F32, "coef", 2)
            nc.vector.tensor_reduce(out=coef[:], in_=sums[g, j][:], op=ALU.add, axis=AX.X)
            nc.gpsimd.tensor_scalar(out=dx[g, j][:], in0=x_sb[g][:, D * j : D * (j + 1)], scalar1=coef[:], scalar2=0.0, op0=ALU.mult, op1=ALU.add)

        dh_tok = {}

        def dh_tile_passes(j, banks, passes):
            for half in range(2):
                if passes[0] == 0:
                    dh_tok[j, half] = bank(banks[half])
                for fq in passes:
                    w_codes, w_scales = w_q[fq, half]
                    z_codes, z_scales = dz_feat_q[4 + fq]
                    cols = slice(P * j, P * (j + 1))
                    nc.tensor.matmul_mx(out=dh_tok[j, half][:], lhsT=z_codes[:, cols].bitcast(E5M2), lhsT_scale=z_scales[:, cols],
                                        rhs=w_codes[:].bitcast(E4M3), rhs_scale=w_scales[:], start=(fq == 0), stop=(fq == 3))

        shift, coefs = {}, {}

        def tile_mean(j):
            shift[j] = sbuf([P, D], F32, "prod", 5)
            sums[1, j] = sbuf([P, 2], F32, "sums", 4)
            for half in range(2):
                nc.vector.scalar_tensor_tensor(out=shift[j][:, halves[half]], in0=dh_tok[j, half][:], scalar=neg_r2[:, 4 + j : 5 + j],
                                               in1=h_raw[1][:, D * j + PASS * half : D * j + PASS * (half + 1)],
                                               op0=ALU.mult, op1=ALU.mult, accum_out=sums[1, j][:, half : half + 1])

        def tile_gain(j):
            dx[1, j] = sbuf([P, D], F32, "grad", 5)
            coefs[j] = sbuf([P, 1], F32, "coef", 2)
            for half in range(2):
                nc.vector.scalar_tensor_tensor(out=dx[1, j][:, halves[half]], in0=dh_tok[j, half][:], scalar=r_sb[:, 4 + j : 5 + j],
                                               in1=gain_wide[:, halves[half]], op0=ALU.mult, op1=ALU.mult)
                if half == 0:
                    nc.vector.tensor_reduce(out=coefs[j][:], in_=sums[1, j][:], op=ALU.add, axis=AX.X)

        def tile_finish(j):
            nc.scalar.activation(out=shift[j][:], in_=x_sb[1][:, D * j : D * (j + 1)], func=ACT.Copy, scale=coefs[j][:])
            for half in range(2):
                part = dx[1, j][:, halves[half]]
                nc.gpsimd.tensor_tensor(out=part, in0=part, in1=shift[j][:, halves[half]], op=ALU.add)
                nc.sync.dma_start(out=dx_hbm[1, j][:, halves[half]], in_=part)

        def last_tile_finish(j):
            for half in range(2):
                part = dx[1, j][:, halves[half]]
                nc.vector.scalar_tensor_tensor(out=part, in0=x_sb[1][:, D * j + PASS * half : D * j + PASS * (half + 1)], scalar=coefs[j][:], in1=part, op0=ALU.mult, op1=ALU.add)
                nc.sync.dma_start(out=dx_hbm[1, j][:, halves[half]], in_=part)

        def norm_finish(g, j):
            slot = slice(4 * g + j, 4 * g + j + 1)
            for half in range(2):
                part = dx[g, j][:, halves[half]]
                nc.vector.scalar_tensor_tensor(out=part, in0=t_tok[g, j, half][:], scalar=r_sb[:, slot], in1=part, op0=ALU.mult, op1=ALU.add)
            nc.sync.dma_start(out=dx_hbm[g, j], in_=dx[g, j][:])

        on_gpsimd = (nc.gpsimd, nc.gpsimd)

        def first_products(n):
            rope_product(n, 0)
            rope_product(n, 1)
            rope_sum(n, 0, on_gpsimd)

        def second_products(n):
            rope_product(n, 2)
            rope_product(n, 3, slice(0, 3))

        def close_chunk(n):
            rope_product(n, 3, slice(3, 4))
            rope_sum(n, 1, on_gpsimd)
            if n + 5 < 8:
                load_grad(n + 5)

        def t_banks_fill(j):
            for half in range(2):
                t_transpose(0, j, half, (7, 2)[half])

        def mean_terms(j):
            for half in range(2):
                norm_mean(0, j, half)

        every_pass = range(4)
        mx_banks = (5, 6, 0)

        whole_turns(0)
        nc.vector.scalar_tensor_tensor(out=neg_r2[:], in0=r_sb[:], scalar=-1.0 / D, in1=r_sb[:], op0=ALU.mult, op1=ALU.mult)
        frac_high(0)
        nc.vector.tensor_tensor(out=neg_r3[:], in0=neg_r2[:], in1=r_sb[:], op=ALU.mult)
        x_normalise(0)
        frac_low(0)
        table_to_psum(0, 0)
        x_normalise(1)
        for part in range(2):
            h_from_x_hat(part)
        for j in range(4):
            h_slot(0, j)
        nc.scalar.activation(out=pos[:, PASS:S], in_=pos[:, 0:PASS], func=ACT.Copy, bias=float(PASS))
        w_transpose(0, 0, (3, 4))
        w_transpose(0, 1, (5, 6))
        nc.scalar.copy(out=gain_col[:], in_=gain_t[:, 0:8])
        load_weight(3)
        for n in range(4):
            if n == 1:
                h_interleave(0, 1)
            first_products(n)
            second_products(n)
            h_slot(1, n)
            if n > 0:
                dz_transpose(n - 1, (3, 4))
                tok_quantize(n - 1)
            if n == 0:
                whole_turns(1)
            w_quantize(n, 0)
            if n == 0:
                frac_high(1)
            w_quantize(n, 1)
            if n == 0:
                frac_low(1)
            if n < 3:
                w_transpose(n + 1, 0, (5, 1))
                w_transpose(n + 1, 1, (3, 4))
            if n in (1, 2):
                h_quantize(0, n - 1)
            if n == 3:
                table_to_psum(1, 1)
                dh_passes(0, 2, 5, range(2))
            close_chunk(n)
            if n > 0:
                feat_quantize(n - 1)
                for k in range(2 if n < 3 else 3):
                    dh_passes(0, k, (6, 7, 5)[k], [n - 1])
        h_interleave(1, 0)
        rope_product(4, 0)
        rope_product(4, 1)
        rope_add(4, 0, nc.gpsimd)
        for k in range(3, 5):
            dh_passes(0, k, (0, 2)[k - 3], range(3))
        dz_transpose(3, (3, 4))
        h_interleave(1, 1)
        second_products(4)
        rope_add(4, 1, nc.vector)
        tok_quantize(3)
        h_quantize(1, 0)
        close_chunk(4)
        feat_quantize(3)
        for k in range(3):
            dh_passes(0, k, None, [3])
        first_products(5)
        for k in range(3, 5):
            dh_passes(0, k, None, [3])
        dh_passes(0, 5, 6, every_pass)
        dz_transpose(4, (3, 4))
        for k in range(6, 8):
            dh_passes(0, k, (5, 0)[k - 6], every_pass)
        t_banks_fill(0)
        second_products(5)
        tok_quantize(4)
        h_quantize(1, 1)
        close_chunk(5)
        for k in range(4):
            dw_block(0, k, mx_banks[(k + 1) % 3])
        rope_product(6, 0)
        mean_terms(0)
        rope_product(6, 1)
        norm_shift(0, 0)
        rope_add(6, 0, nc.gpsimd)
        dz_transpose(5, (3, 4))
        for k in range(4, 8):
            dw_block(0, k, mx_banks[(k + 1) % 3])
        second_products(6)
        norm_finish(0, 0)
        t_banks_fill(1)
        rope_add(6, 1, nc.vector)
        feat_quantize(4)
        tok_quantize(5)
        close_chunk(6)
        feat_quantize(5)
        for k in range(4):
            dw_block(1, k, mx_banks[k % 3])
        rope_product(7, 0)
        mean_terms(1)
        rope_product(7, 1, slice(0, 3))
        norm_shift(0, 1)
        dz_transpose(6, (3, 4))
        for k in range(4, 8):
            dw_block(1, k, mx_banks[k % 3])
        rope_product(7, 2)
        tok_quantize(6)
        rope_product(7, 1, slice(3, 4))
        rope_sum(7, 0, on_gpsimd)
        norm_finish(0, 1)
        t_banks_fill(2)
        for k in range(5):
            dw_block(2, k, mx_banks[(k + 2) % 3])
        rope_product(7, 3)
        mean_terms(2)
        rope_sum(7, 1, (nc.vector, nc.vector))
        feat_quantize(6)
        tok_quantize(7)
        norm_shift(0, 2)
        dz_transpose(7, (3, 4), (nc.scalar.copy, nc.vector.tensor_copy))
        dw_block(2, 5, 6)
        dh_tile_passes(0, (1, 5), range(3))
        feat_quantize(7)
        norm_finish(0, 2)
        dh_tile_passes(0, None, [3])
        t_banks_fill(3)
        rest = [(2, k) for k in range(6, 8)] + [(3, k) for k in range(8)]
        for fq, k in rest[0:2]:
            dw_block(fq, k, (3, 4)[k % 2])
        dh_tile_passes(1, (6, 0), every_pass)
        tile_mean(0)
        tile_gain(0)
        mean_terms(3)
        norm_shift(0, 3)
        tile_finish(0)
        for fq, k in rest[2:6]:
            dw_block(fq, k, (3, 4)[k % 2])
        dh_tile_passes(2, (1, 5), every_pass)
        tile_mean(1)
        tile_gain(1)
        norm_finish(0, 3)
        tile_finish(1)
        for fq, k in rest[6:8]:
            dw_block(fq, k, (3, 4)[k % 2])
        dh_tile_passes(3, (6, 0), every_pass)
        for fq, k in rest[8:10]:
            dw_block(fq, k, (3, 4)[k % 2])
        tile_mean(2)
        tile_gain(2)
        last_tile_finish(2)
        tile_mean(3)
        tile_gain(3)
        last_tile_finish(3)
